import numpy as np
import ml_dtypes


def mxq(x, axis, fmt="e4m3"):
    dtype, down = {"e4m3": (ml_dtypes.float8_e4m3fn, 7), "e5m2": (ml_dtypes.float8_e5m2, 14)}[fmt]
    v = np.moveaxis(np.asarray(x, np.float32).astype(ml_dtypes.bfloat16).astype(np.float64), axis, -1)
    blocks = v.reshape(v.shape[:-1] + (-1, 32))
    amax = np.abs(blocks).max(-1, keepdims=True)
    byte = np.maximum(np.where(amax > 0, np.frexp(amax)[1] - 1 + 127, 0) - down, 1)
    scale = np.exp2(byte - 127.0)
    codes = (blocks / scale).astype(np.float32).astype(dtype).astype(np.float64)
    return np.moveaxis((codes * scale).reshape(v.shape), -1, axis)


WIDE = False


def mx_kscale(k):
    if not WIDE:
        return np.ones(k)
    levels = np.array([20, -20, 10, -10, 0])
    a = np.random.permutation(np.resize(levels, k // 512 * 4)).reshape(k // 512, 4)
    idx = np.arange(k)
    return np.exp2(a[idx // 512, idx % 128 // 32])


BF16 = ml_dtypes.bfloat16


def bf(x):
    return np.asarray(x, np.float32).astype(BF16)


def f64(x):
    return np.asarray(x).astype(np.float64)


S, H, E, P, C = 1024, 256, 416, 64, 32
IN0 = E + P + C + 4 * H


def sigmoid(v):
    return 1.0 / (1.0 + np.exp(-v))


def setup_inputs():
    n = np.random.standard_normal
    s = mx_kscale(S)[:, None]
    streams = ("hn_chunks", "hn_tags", "x", "tags", "chunks")
    d0 = {"hn_chunks": bf(n((S, 2 * H))), "hn_tags": bf(n((S, 2 * H))), "x": bf(n((S, E))),
          "tags": bf(n((S, P))), "chunks": bf(n((S, C)))}
    d = {"h0": bf(n((2, S, H))), "c0": bf(n((2, S, H)))}
    for k in ("f", "b"):
        d["wih_" + k] = bf(n((4 * H, IN0)) / np.sqrt(IN0))
        d["whh_" + k] = bf(n((4 * H, H)) * 0.7 / np.sqrt(H))
        d["bih_" + k] = bf(n(4 * H) * 0.2)
        d["bhh_" + k] = bf(n(4 * H) * 0.2)
    g = bf(n((S, 2 * H)) * np.exp2(np.random.randint(-12, 1, (S, 1))) * 4.0 / s)
    gt0 = np.concatenate([f64(d0[k]) for k in streams], axis=1)
    gf = gt0 @ f64(d["wih_f"]).T + f64(d["bih_f"]) + f64(d["h0"])[0] @ f64(d["whh_f"]).T + f64(d["bhh_f"])
    res = {k: bf(f64(d0[k]) * s) for k in streams}
    res.update(d)
    res["gf"] = np.asarray(gf, np.float32)
    res["grad_out"] = g
    return res


def reference(hn_chunks, hn_tags, x, tags, chunks, h0, c0, wih_f, whh_f, bih_f, bhh_f, wih_b, whh_b, bih_b, bhh_b, gf, grad_out):
    gt = np.concatenate([f64(hn_chunks), f64(hn_tags), f64(x), f64(tags), f64(chunks)], axis=1)
    go = f64(grad_out)[:, :H]
    c = f64(c0)[0]
    i, f, gg, o = np.split(f64(gf), 4, axis=-1)
    si, sf, so, tg = sigmoid(i), sigmoid(f), sigmoid(o), np.tanh(gg)
    tc = np.tanh(sf * c + si * tg)
    dc2 = go * so * (1.0 - tc * tc)
    di = dc2 * tg * si * (1.0 - si)
    df = dc2 * c * sf * (1.0 - sf)
    dgg = dc2 * si * (1.0 - tg * tg)
    do = go * tc * so * (1.0 - so)
    dg = np.concatenate([di, df, dgg, do], axis=1)
    return mxq(dg, 0, "e5m2").T @ mxq(gt, 0, "e4m3")

@@ -1,0 +1,219 @@
+import concourse.mybir as mybir
+
+F32 = mybir.dt.float32
+BF16 = mybir.dt.bfloat16
+U32 = mybir.dt.uint32
+U8 = mybir.dt.uint8
+E4M3_X4 = mybir.dt.float8_e4m3fn_x4
+E5M2_X4 = mybir.dt.float8_e5m2_x4
+FUNC = mybir.ActivationFunctionType
+ALU = mybir.AluOpType
+
+P = 128
+PACK = 4
+K_PASS = P * PACK
+TOKENS = 1024
+PASSES = TOKENS // K_PASS
+ROWS = PASSES * PACK
+H = 256
+GATE_I, GATE_F, GATE_G, GATE_O = 0, 1, 2, 3
+GATES = 4
+M_TILE = 128
+H_BLOCKS = H // M_TILE
+N_TILE = 512
+N_TILES = 3
+RUN = 4
+
+FLOPS = 2 * TOKENS * (GATES * H) * (N_TILES * N_TILE)
+BYTES = (
+    TOKENS * N_TILES * N_TILE * 2
+    + TOKENS * GATES * H * 4
+    + 2 * TOKENS * H * 2
+    + GATES * H * N_TILES * N_TILE * 4
+)
+
+
+def by_column(rows_first):
+    return rows_first.rearrange("p t (q i) -> p q t i", i=RUN)
+
+
+def by_column_grouped(columns_first):
+    return columns_first.rearrange("p (q i) t -> p q t i", i=RUN)
+
+
+def tile_dependency_pa_v_kernel(
+    tc,
+    hn_chunks,
+    hn_tags,
+    x,
+    tags,
+    chunks,
+    h0,
+    c0,
+    wih_f,
+    whh_f,
+    bih_f,
+    bhh_f,
+    wih_b,
+    whh_b,
+    bih_b,
+    bhh_b,
+    gf,
+    grad_out,
+    out,
+):
+    nc = tc.nc
+    with (
+        tc.tile_pool(name="resident", bufs=1) as resident,
+        tc.tile_pool(name="gates", bufs=2) as gates,
+        tc.tile_pool(name="chain", bufs=1) as chain,
+        tc.tile_pool(name="grouped", bufs=2) as grouped_pool,
+        tc.tile_pool(name="stage", bufs=6) as stage,
+        tc.psum_pool(name="psum", bufs=8) as psum,
+    ):
+        gf_sb = [resident.tile([P, ROWS, H], F32, name="gf_sb%d" % g) for g in range(GATES)]
+        cell_sb = resident.tile([P, ROWS, H], BF16, name="cell_sb")
+        go_sb = resident.tile([P, ROWS, H], BF16, name="go_sb")
+        gt_sb = [resident.tile([P, ROWS, N_TILE], BF16, name="gt_sb%d" % n) for n in range(N_TILES)]
+
+        def load(dst, c, dst_cols, src):
+            nc.sync.dma_start(
+                out=dst[:, c * PACK : (c + 1) * PACK, dst_cols],
+                in_=src[c * K_PASS : (c + 1) * K_PASS, :].rearrange("(p j) w -> p j w", j=PACK),
+            )
+
+        whole_gate = slice(0, H)
+        for c in range(PASSES):
+            load(gf_sb[GATE_I], c, whole_gate, gf[:, GATE_I * H : (GATE_I + 1) * H])
+            load(gf_sb[GATE_G], c, whole_gate, gf[:, GATE_G * H : (GATE_G + 1) * H])
+            load(gf_sb[GATE_F], c, whole_gate, gf[:, GATE_F * H : (GATE_F + 1) * H])
+            load(cell_sb, c, whole_gate, c0[0, :, :])
+            load(gf_sb[GATE_O], c, whole_gate, gf[:, GATE_O * H : (GATE_O + 1) * H])
+            load(go_sb, c, whole_gate, grad_out[:, 0:H])
+        for c in range(PASSES):
+            load(gt_sb[0], c, slice(0, N_TILE), hn_chunks)
+            load(gt_sb[1], c, slice(0, N_TILE), hn_tags)
+            load(gt_sb[2], c, slice(0, 416), x)
+            load(gt_sb[2], c, slice(416, 480), tags)
+            load(gt_sb[2], c, slice(480, 512), chunks)
+
+        gt_codes = resident.tile([P, PASSES, N_TILES, N_TILE], U32, name="gt_codes", align_bytes=64)
+        gt_scales = resident.tile([P, PASSES, N_TILES, N_TILE], U8, name="gt_scales", align_bytes=64)
+        dg_codes = resident.tile([P, H_BLOCKS, GATES, PASSES, M_TILE], U32, name="dg_codes", align_bytes=64)
+        dg_scales = resident.tile([P, H_BLOCKS, GATES, PASSES, M_TILE], U8, name="dg_scales", align_bytes=64)
+
+        def quantise_gt(c, n):
+            gt_grouped = grouped_pool.tile([P, N_TILE, PACK], BF16, name="gt_grouped", align_bytes=64)
+            rows = gt_sb[n][:, c * PACK : (c + 1) * PACK, :]
+            if n == 0:
+                nc.vector.tensor_copy(out=by_column_grouped(gt_grouped[:]), in_=by_column(rows))
+            else:
+                nc.scalar.copy(out=by_column_grouped(gt_grouped[:]), in_=by_column(rows))
+            nc.vector.quantize_mx(
+                out=gt_codes[:, c, n, :].bitcast(E4M3_X4),
+                scales=gt_scales[:, c, n, :],
+                in_=gt_grouped[:].rearrange("p w t -> p (w t)"),
+            )
+
+        def gate_gradients(hb, first_pass, n_passes):
+            rows = slice(first_pass * PACK, (first_pass + n_passes) * PACK)
+            cols = slice(hb * M_TILE, (hb + 1) * M_TILE)
+            shape = [P, n_passes * PACK, M_TILE]
+
+            def activation(name, func, in_, scale=1.0):
+                result = gates.tile(shape, F32, name=name)
+                nc.scalar.activation(out=result[:], in_=in_, func=func, scale=scale)
+                return result
+
+            def product(name, in0, in1):
+                result = chain.tile(shape, F32, name=name)
+                nc.vector.tensor_tensor(out=result[:], in0=in0, in1=in1, op=ALU.mult)
+                return result
+
+            def minus_one_times(name, in0, in1):
+                result = chain.tile(shape, F32, name=name)
+                nc.vector.scalar_tensor_tensor(
+                    out=result[:], in0=in0, scalar=1.0, in1=in1, op0=ALU.subtract, op1=ALU.mult
+                )
+                return result
+
+            def finish(g, in0, in1):
+                dg_grouped = grouped_pool.tile([P, n_passes, M_TILE, PACK], BF16, name="dg_grouped%d" % g, align_bytes=64)
+                for k in range(n_passes):
+                    k_rows = slice(k * PACK, (k + 1) * PACK)
+                    nc.vector.tensor_tensor(
+                        out=by_column_grouped(dg_grouped[:, k, :, :]),
+                        in0=by_column(in0[:, k_rows, :]),
+                        in1=by_column(in1[:, k_rows, :]),
+                        op=ALU.mult,
+                    )
+                return dg_grouped
+
+            def quantise_dg(g, dg_grouped):
+                passes = slice(first_pass, first_pass + n_passes)
+                nc.vector.quantize_mx(
+                    out=dg_codes[:, hb, g, passes, :].rearrange("p c m -> p (c m)").bitcast(E5M2_X4),
+                    scales=dg_scales[:, hb, g, passes, :].rearrange("p c m -> p (c m)"),
+                    in_=dg_grouped[:].rearrange("p c m t -> p (c m t)"),
+                )
+
+            si = activation("si", FUNC.Sigmoid, gf_sb[GATE_I][:, rows, cols])
+            tg = activation("tg", FUNC.Tanh, gf_sb[GATE_G][:, rows, cols])
+            sf = activation("sf", FUNC.Sigmoid, gf_sb[GATE_F][:, rows, cols])
+            so = activation("so", FUNC.Sigmoid, gf_sb[GATE_O][:, rows, cols])
+            tg2 = activation("tg2", FUNC.Square, tg[:])
+
+            input_part = product("input_part", si[:], tg[:])
+            forget_part = product("forget_part", sf[:], cell_sb[:, rows, cols])
+            c2 = chain.tile(shape, F32, name="c2")
+            nc.vector.tensor_tensor(out=c2[:], in0=input_part[:], in1=forget_part[:], op=ALU.add)
+            minus_tc = activation("minus_tc", FUNC.Tanh, c2[:], scale=-1.0)
+            tc2 = activation("tc2", FUNC.Square, minus_tc[:])
+
+            go_so = product("go_so", so[:], go_sb[:, rows, cols])
+            minus_do_tc = minus_one_times("minus_do_tc", so[:], go_so[:])
+            do_grouped = finish(GATE_O, minus_do_tc, minus_tc)
+            minus_dc2 = minus_one_times("minus_dc2", tc2[:], go_so[:])
+            minus_i = minus_one_times("minus_i", si[:], input_part[:])
+            quantise_dg(GATE_O, do_grouped)
+            di_grouped = finish(GATE_I, minus_i, minus_dc2)
+            minus_f = minus_one_times("minus_f", sf[:], forget_part[:])
+            quantise_dg(GATE_I, di_grouped)
+            df_grouped = finish(GATE_F, minus_f, minus_dc2)
+            minus_g = minus_one_times("minus_g", tg2[:], si[:])
+            quantise_dg(GATE_F, df_grouped)
+            dgg_grouped = finish(GATE_G, minus_g, minus_dc2)
+            quantise_dg(GATE_G, dgg_grouped)
+
+        def multiply_and_store(hb, g):
+            first_row = g * H + hb * M_TILE
+            for n in range(N_TILES):
+                acc = psum.tile([M_TILE, N_TILE], F32, name="acc")
+                for c in range(PASSES):
+                    nc.tensor.matmul_mx(
+                        out=acc[:],
+                        lhsT=dg_codes[:, hb, g, c, :].bitcast(E5M2_X4),
+                        lhsT_scale=dg_scales[:, hb, g, c, :],
+                        rhs=gt_codes[:, c, n, :].bitcast(E4M3_X4),
+                        rhs_scale=gt_scales[:, c, n, :],
+                        start=(c == 0),
+                        stop=(c == PASSES - 1),
+                    )
+                result = stage.tile([M_TILE, N_TILE], F32, name="result")
+                nc.scalar.copy(out=result[:], in_=acc[:])
+                nc.sync.dma_start(
+                    out=out[first_row : first_row + M_TILE, n * N_TILE : (n + 1) * N_TILE], in_=result[:]
+                )
+
+        gates_as_they_finish = (GATE_O, GATE_I, GATE_F, GATE_G)
+
+        gate_gradients(0, 0, 1)
+        gate_gradients(0, 1, 1)
+        for c in range(PASSES):
+            for n in range(N_TILES):
+                quantise_gt(c, n)
+        for g in gates_as_they_finish:
+            multiply_and_store(0, g)
+        gate_gradients(1, 0, PASSES)
+        for g in gates_as_they_finish:
+            multiply_and_store(1, g)

@@ -1,4 +1,5 @@
 import concourse.mybir as mybir
+from concourse.masks import make_identity
 
 F32 = mybir.dt.float32
 BF16 = mybir.dt.bfloat16
@@ -68,10 +69,15 @@ def tile_dependency_pa_v_kernel(
         tc.tile_pool(name="gates", bufs=2) as gates,
         tc.tile_pool(name="chain", bufs=1) as chain,
         tc.tile_pool(name="grouped", bufs=2) as grouped_pool,
-        tc.tile_pool(name="stage", bufs=6) as stage,
-        tc.psum_pool(name="psum", bufs=8) as psum,
+        tc.tile_pool(name="gt_grouped", bufs=3) as gt_grouped_pool,
+        tc.tile_pool(name="stage", bufs=8) as stage,
+        tc.psum_pool(name="psum", bufs=6) as psum,
+        tc.psum_pool(name="psum_c2", bufs=2) as psum_c2,
     ):
-        gf_sb = [resident.tile([P, ROWS, H], F32, name="gf_sb%d" % g) for g in range(GATES)]
+        gf_sb = [
+            [resident.tile([P, ROWS, M_TILE], F32, name="gf_sb%d_%d" % (g, hb)) for hb in range(H_BLOCKS)]
+            for g in range(GATES)
+        ]
         cell_sb = resident.tile([P, ROWS, H], BF16, name="cell_sb")
         go_sb = resident.tile([P, ROWS, H], BF16, name="go_sb")
         gt_sb = [resident.tile([P, ROWS, N_TILE], BF16, name="gt_sb%d" % n) for n in range(N_TILES)]
@@ -82,20 +88,41 @@ def tile_dependency_pa_v_kernel(
                 in_=src[c * K_PASS : (c + 1) * K_PASS, :].rearrange("(p j) w -> p j w", j=PACK),
             )
 
-        whole_gate = slice(0, H)
-        for c in range(PASSES):
-            load(gf_sb[GATE_I], c, whole_gate, gf[:, GATE_I * H : (GATE_I + 1) * H])
-            load(gf_sb[GATE_G], c, whole_gate, gf[:, GATE_G * H : (GATE_G + 1) * H])
-            load(gf_sb[GATE_F], c, whole_gate, gf[:, GATE_F * H : (GATE_F + 1) * H])
-            load(cell_sb, c, whole_gate, c0[0, :, :])
-            load(gf_sb[GATE_O], c, whole_gate, gf[:, GATE_O * H : (GATE_O + 1) * H])
-            load(go_sb, c, whole_gate, grad_out[:, 0:H])
-        for c in range(PASSES):
-            load(gt_sb[0], c, slice(0, N_TILE), hn_chunks)
-            load(gt_sb[1], c, slice(0, N_TILE), hn_tags)
-            load(gt_sb[2], c, slice(0, 416), x)
-            load(gt_sb[2], c, slice(416, 480), tags)
-            load(gt_sb[2], c, slice(480, 512), chunks)
+        def load_gate(g, hb, c):
+            first_col = g * H + hb * M_TILE
+            load(gf_sb[g][hb], c, slice(0, M_TILE), gf[:, first_col : first_col + M_TILE])
+
+        def load_gt(c, n):
+            if n == 0:
+                load(gt_sb[0], c, slice(0, N_TILE), hn_chunks)
+            elif n == 1:
+                load(gt_sb[1], c, slice(0, N_TILE), hn_tags)
+            else:
+                load(gt_sb[2], c, slice(0, 416), x)
+                load(gt_sb[2], c, slice(416, 480), tags)
+                load(gt_sb[2], c, slice(480, 512), chunks)
+
+        def load_first_block(c):
+            load_gate(GATE_I, 0, c)
+            load_gate(GATE_G, 0, c)
+            load_gate(GATE_F, 0, c)
+            load(cell_sb, c, slice(0, H), c0[0, :, :])
+            load_gate(GATE_O, 0, c)
+            load(go_sb, c, slice(0, H), grad_out[:, 0:H])
+
+        load_first_block(0)
+        load_gt(0, 0)
+        load_gt(0, 1)
+        load_first_block(1)
+        load_gt(0, 2)
+        for n in range(N_TILES):
+            load_gt(1, n)
+        for g in (GATE_I, GATE_G, GATE_F, GATE_O):
+            for c in range(PASSES):
+                load_gate(g, 1, c)
+
+        identity = resident.tile([P, P], F32, name="identity")
+        make_identity(nc, identity[:])
 
         gt_codes = resident.tile([P, PASSES, N_TILES, N_TILE], U32, name="gt_codes", align_bytes=64)
         gt_scales = resident.tile([P, PASSES, N_TILES, N_TILE], U8, name="gt_scales", align_bytes=64)
@@ -103,9 +130,9 @@ def tile_dependency_pa_v_kernel(
         dg_scales = resident.tile([P, H_BLOCKS, GATES, PASSES, M_TILE], U8, name="dg_scales", align_bytes=64)
 
         def quantise_gt(c, n):
-            gt_grouped = grouped_pool.tile([P, N_TILE, PACK], BF16, name="gt_grouped", align_bytes=64)
+            gt_grouped = gt_grouped_pool.tile([P, N_TILE, PACK], BF16, name="gt_grouped", align_bytes=64)
             rows = gt_sb[n][:, c * PACK : (c + 1) * PACK, :]
-            if n == 0:
+            if c * N_TILES + n >= 4:
                 nc.vector.tensor_copy(out=by_column_grouped(gt_grouped[:]), in_=by_column(rows))
             else:
                 nc.scalar.copy(out=by_column_grouped(gt_grouped[:]), in_=by_column(rows))
@@ -157,17 +184,27 @@ def tile_dependency_pa_v_kernel(
                     in_=dg_grouped[:].rearrange("p c m t -> p (c m t)"),
                 )
 
-            si = activation("si", FUNC.Sigmoid, gf_sb[GATE_I][:, rows, cols])
-            tg = activation("tg", FUNC.Tanh, gf_sb[GATE_G][:, rows, cols])
-            sf = activation("sf", FUNC.Sigmoid, gf_sb[GATE_F][:, rows, cols])
-            so = activation("so", FUNC.Sigmoid, gf_sb[GATE_O][:, rows, cols])
+            si = activation("si", FUNC.Sigmoid, gf_sb[GATE_I][hb][:, rows, :])
+            tg = activation("tg", FUNC.Tanh, gf_sb[GATE_G][hb][:, rows, :])
+            sf = activation("sf", FUNC.Sigmoid, gf_sb[GATE_F][hb][:, rows, :])
+            so = activation("so", FUNC.Sigmoid, gf_sb[GATE_O][hb][:, rows, :])
             tg2 = activation("tg2", FUNC.Square, tg[:])
 
             input_part = product("input_part", si[:], tg[:])
             forget_part = product("forget_part", sf[:], cell_sb[:, rows, cols])
-            c2 = chain.tile(shape, F32, name="c2")
-            nc.vector.tensor_tensor(out=c2[:], in0=input_part[:], in1=forget_part[:], op=ALU.add)
-            minus_tc = activation("minus_tc", FUNC.Tanh, c2[:], scale=-1.0)
+            minus_tc = gates.tile(shape, F32, name="minus_tc")
+            for k in range(n_passes):
+                k_rows = slice(k * PACK, (k + 1) * PACK)
+                c2 = psum_c2.tile([P, PACK, M_TILE], F32, name="c2")
+                for part in (input_part, forget_part):
+                    nc.tensor.matmul(
+                        out=c2[:].rearrange("p j h -> p (j h)"),
+                        lhsT=identity[:],
+                        rhs=part[:, k_rows, :].rearrange("p j h -> p (j h)"),
+                        start=(part is input_part),
+                        stop=(part is forget_part),
+                    )
+                nc.scalar.activation(out=minus_tc[:, k_rows, :], in_=c2[:], func=FUNC.Tanh, scale=-1.0)
             tc2 = activation("tc2", FUNC.Square, minus_tc[:])
 
             go_so = product("go_so", so[:], go_sb[:, rows, cols])
@@ -200,7 +237,10 @@ def tile_dependency_pa_v_kernel(
                         stop=(c == PASSES - 1),
                     )
                 result = stage.tile([M_TILE, N_TILE], F32, name="result")
-                nc.scalar.copy(out=result[:], in_=acc[:])
+                if hb == H_BLOCKS - 1 and n == 1:
+                    nc.vector.tensor_copy(out=result[:], in_=acc[:])
+                else:
+                    nc.scalar.copy(out=result[:], in_=acc[:])
                 nc.sync.dma_start(
                     out=out[first_row : first_row + M_TILE, n * N_TILE : (n + 1) * N_TILE], in_=result[:]
                 )
@@ -208,12 +248,13 @@ def tile_dependency_pa_v_kernel(
         gates_as_they_finish = (GATE_O, GATE_I, GATE_F, GATE_G)
 
         gate_gradients(0, 0, 1)
+        quantise_gt(0, 0)
+        quantise_gt(0, 1)
         gate_gradients(0, 1, 1)
-        for c in range(PASSES):
-            for n in range(N_TILES):
-                quantise_gt(c, n)
-        for g in gates_as_they_finish:
-            multiply_and_store(0, g)
+        quantise_gt(0, 2)
+        for n in range(N_TILES):
+            quantise_gt(1, n)
         gate_gradients(1, 0, PASSES)
-        for g in gates_as_they_finish:
-            multiply_and_store(1, g)
+        for hb in range(H_BLOCKS):
+            for g in gates_as_they_finish:
+                multiply_and_store(hb, g)

@@ -1,5 +1,4 @@
 import concourse.mybir as mybir
-from concourse.masks import make_identity
 
 F32 = mybir.dt.float32
 BF16 = mybir.dt.bfloat16
@@ -71,13 +70,9 @@ def tile_dependency_pa_v_kernel(
         tc.tile_pool(name="grouped", bufs=2) as grouped_pool,
         tc.tile_pool(name="gt_grouped", bufs=3) as gt_grouped_pool,
         tc.tile_pool(name="stage", bufs=8) as stage,
-        tc.psum_pool(name="psum", bufs=6) as psum,
-        tc.psum_pool(name="psum_c2", bufs=2) as psum_c2,
+        tc.psum_pool(name="psum", bufs=8) as psum,
     ):
-        gf_sb = [
-            [resident.tile([P, ROWS, M_TILE], F32, name="gf_sb%d_%d" % (g, hb)) for hb in range(H_BLOCKS)]
-            for g in range(GATES)
-        ]
+        gf_sb = [resident.tile([P, ROWS, H], F32, name="gf_sb%d" % g) for g in range(GATES)]
         cell_sb = resident.tile([P, ROWS, H], BF16, name="cell_sb")
         go_sb = resident.tile([P, ROWS, H], BF16, name="go_sb")
         gt_sb = [resident.tile([P, ROWS, N_TILE], BF16, name="gt_sb%d" % n) for n in range(N_TILES)]
@@ -88,41 +83,20 @@ def tile_dependency_pa_v_kernel(
                 in_=src[c * K_PASS : (c + 1) * K_PASS, :].rearrange("(p j) w -> p j w", j=PACK),
             )
 
-        def load_gate(g, hb, c):
-            first_col = g * H + hb * M_TILE
-            load(gf_sb[g][hb], c, slice(0, M_TILE), gf[:, first_col : first_col + M_TILE])
-
-        def load_gt(c, n):
-            if n == 0:
-                load(gt_sb[0], c, slice(0, N_TILE), hn_chunks)
-            elif n == 1:
-                load(gt_sb[1], c, slice(0, N_TILE), hn_tags)
-            else:
-                load(gt_sb[2], c, slice(0, 416), x)
-                load(gt_sb[2], c, slice(416, 480), tags)
-                load(gt_sb[2], c, slice(480, 512), chunks)
-
-        def load_first_block(c):
-            load_gate(GATE_I, 0, c)
-            load_gate(GATE_G, 0, c)
-            load_gate(GATE_F, 0, c)
-            load(cell_sb, c, slice(0, H), c0[0, :, :])
-            load_gate(GATE_O, 0, c)
-            load(go_sb, c, slice(0, H), grad_out[:, 0:H])
-
-        load_first_block(0)
-        load_gt(0, 0)
-        load_gt(0, 1)
-        load_first_block(1)
-        load_gt(0, 2)
-        for n in range(N_TILES):
-            load_gt(1, n)
-        for g in (GATE_I, GATE_G, GATE_F, GATE_O):
-            for c in range(PASSES):
-                load_gate(g, 1, c)
-
-        identity = resident.tile([P, P], F32, name="identity")
-        make_identity(nc, identity[:])
+        whole_gate = slice(0, H)
+        for c in range(PASSES):
+            load(gf_sb[GATE_I], c, whole_gate, gf[:, GATE_I * H : (GATE_I + 1) * H])
+            load(gf_sb[GATE_G], c, whole_gate, gf[:, GATE_G * H : (GATE_G + 1) * H])
+            load(gf_sb[GATE_F], c, whole_gate, gf[:, GATE_F * H : (GATE_F + 1) * H])
+            load(cell_sb, c, whole_gate, c0[0, :, :])
+            load(gf_sb[GATE_O], c, whole_gate, gf[:, GATE_O * H : (GATE_O + 1) * H])
+            load(go_sb, c, whole_gate, grad_out[:, 0:H])
+        for c in range(PASSES):
+            load(gt_sb[0], c, slice(0, N_TILE), hn_chunks)
+            load(gt_sb[1], c, slice(0, N_TILE), hn_tags)
+            load(gt_sb[2], c, slice(0, 416), x)
+            load(gt_sb[2], c, slice(416, 480), tags)
+            load(gt_sb[2], c, slice(480, 512), chunks)
 
         gt_codes = resident.tile([P, PASSES, N_TILES, N_TILE], U32, name="gt_codes", align_bytes=64)
         gt_scales = resident.tile([P, PASSES, N_TILES, N_TILE], U8, name="gt_scales", align_bytes=64)
@@ -184,34 +158,24 @@ def tile_dependency_pa_v_kernel(
                     in_=dg_grouped[:].rearrange("p c m t -> p (c m t)"),
                 )
 
-            si = activation("si", FUNC.Sigmoid, gf_sb[GATE_I][hb][:, rows, :])
-            tg = activation("tg", FUNC.Tanh, gf_sb[GATE_G][hb][:, rows, :])
-            sf = activation("sf", FUNC.Sigmoid, gf_sb[GATE_F][hb][:, rows, :])
-            so = activation("so", FUNC.Sigmoid, gf_sb[GATE_O][hb][:, rows, :])
+            si = activation("si", FUNC.Sigmoid, gf_sb[GATE_I][:, rows, cols])
+            tg = activation("tg", FUNC.Tanh, gf_sb[GATE_G][:, rows, cols])
+            sf = activation("sf", FUNC.Sigmoid, gf_sb[GATE_F][:, rows, cols])
             tg2 = activation("tg2", FUNC.Square, tg[:])
+            so = activation("so", FUNC.Sigmoid, gf_sb[GATE_O][:, rows, cols])
 
             input_part = product("input_part", si[:], tg[:])
             forget_part = product("forget_part", sf[:], cell_sb[:, rows, cols])
-            minus_tc = gates.tile(shape, F32, name="minus_tc")
-            for k in range(n_passes):
-                k_rows = slice(k * PACK, (k + 1) * PACK)
-                c2 = psum_c2.tile([P, PACK, M_TILE], F32, name="c2")
-                for part in (input_part, forget_part):
-                    nc.tensor.matmul(
-                        out=c2[:].rearrange("p j h -> p (j h)"),
-                        lhsT=identity[:],
-                        rhs=part[:, k_rows, :].rearrange("p j h -> p (j h)"),
-                        start=(part is input_part),
-                        stop=(part is forget_part),
-                    )
-                nc.scalar.activation(out=minus_tc[:, k_rows, :], in_=c2[:], func=FUNC.Tanh, scale=-1.0)
+            minus_i = minus_one_times("minus_i", si[:], input_part[:])
+            c2 = chain.tile(shape, F32, name="c2")
+            nc.vector.tensor_tensor(out=c2[:], in0=input_part[:], in1=forget_part[:], op=ALU.add)
+            minus_tc = activation("minus_tc", FUNC.Tanh, c2[:], scale=-1.0)
             tc2 = activation("tc2", FUNC.Square, minus_tc[:])
 
             go_so = product("go_so", so[:], go_sb[:, rows, cols])
             minus_do_tc = minus_one_times("minus_do_tc", so[:], go_so[:])
             do_grouped = finish(GATE_O, minus_do_tc, minus_tc)
             minus_dc2 = minus_one_times("minus_dc2", tc2[:], go_so[:])
-            minus_i = minus_one_times("minus_i", si[:], input_part[:])
             quantise_dg(GATE_O, do_grouped)
             di_grouped = finish(GATE_I, minus_i, minus_dc2)
             minus_f = minus_one_times("minus_f", sf[:], forget_part[:])
@@ -237,7 +201,7 @@ def tile_dependency_pa_v_kernel(
                         stop=(c == PASSES - 1),
                     )
                 result = stage.tile([M_TILE, N_TILE], F32, name="result")
-                if hb == H_BLOCKS - 1 and n == 1:
+                if hb == H_BLOCKS - 1 and g == gates_as_they_finish[-1]:
                     nc.vector.tensor_copy(out=result[:], in_=acc[:])
                 else:
                     nc.scalar.copy(out=result[:], in_=acc[:])
@@ -248,12 +212,10 @@ def tile_dependency_pa_v_kernel(
         gates_as_they_finish = (GATE_O, GATE_I, GATE_F, GATE_G)
 
         gate_gradients(0, 0, 1)
-        quantise_gt(0, 0)
-        quantise_gt(0, 1)
         gate_gradients(0, 1, 1)
-        quantise_gt(0, 2)
-        for n in range(N_TILES):
-            quantise_gt(1, n)
+        for c in range(PASSES):
+            for n in range(N_TILES):
+                quantise_gt(c, n)
         gate_gradients(1, 0, PASSES)
         for hb in range(H_BLOCKS):
             for g in gates_as_they_finish:

@@ -106,7 +106,7 @@ def tile_dependency_pa_v_kernel(
         def quantise_gt(c, n):
             gt_grouped = gt_grouped_pool.tile([P, N_TILE, PACK], BF16, name="gt_grouped", align_bytes=64)
             rows = gt_sb[n][:, c * PACK : (c + 1) * PACK, :]
-            if c * N_TILES + n >= 4:
+            if c * N_TILES + n >= 5:
                 nc.vector.tensor_copy(out=by_column_grouped(gt_grouped[:]), in_=by_column(rows))
             else:
                 nc.scalar.copy(out=by_column_grouped(gt_grouped[:]), in_=by_column(rows))

@@ -75,7 +75,10 @@ def tile_dependency_pa_v_kernel(
         gf_sb = [resident.tile([P, ROWS, H], F32, name="gf_sb%d" % g) for g in range(GATES)]
         cell_sb = resident.tile([P, ROWS, H], BF16, name="cell_sb")
         go_sb = resident.tile([P, ROWS, H], BF16, name="go_sb")
-        gt_sb = [resident.tile([P, ROWS, N_TILE], BF16, name="gt_sb%d" % n) for n in range(N_TILES)]
+        streams = (hn_chunks, hn_tags, x, tags, chunks)
+        widths = [stream.shape[1] for stream in streams]
+        first_cols = [sum(widths[:s]) for s in range(len(streams))]
+        stream_sb = [resident.tile([P, ROWS, widths[s]], BF16, name="stream_sb%d" % s) for s in range(len(streams))]
 
         def load(dst, c, dst_cols, src):
             nc.sync.dma_start(
@@ -92,11 +95,8 @@ def tile_dependency_pa_v_kernel(
             load(gf_sb[GATE_O], c, whole_gate, gf[:, GATE_O * H : (GATE_O + 1) * H])
             load(go_sb, c, whole_gate, grad_out[:, 0:H])
         for c in range(PASSES):
-            load(gt_sb[0], c, slice(0, N_TILE), hn_chunks)
-            load(gt_sb[1], c, slice(0, N_TILE), hn_tags)
-            load(gt_sb[2], c, slice(0, 416), x)
-            load(gt_sb[2], c, slice(416, 480), tags)
-            load(gt_sb[2], c, slice(480, 512), chunks)
+            for s in range(len(streams)):
+                load(stream_sb[s], c, slice(0, widths[s]), streams[s])
 
         gt_codes = resident.tile([P, PASSES, N_TILES, N_TILE], U32, name="gt_codes", align_bytes=64)
         gt_scales = resident.tile([P, PASSES, N_TILES, N_TILE], U8, name="gt_scales", align_bytes=64)
@@ -105,16 +105,35 @@ def tile_dependency_pa_v_kernel(
 
         def quantise_gt(c, n):
             gt_grouped = gt_grouped_pool.tile([P, N_TILE, PACK], BF16, name="gt_grouped", align_bytes=64)
-            rows = gt_sb[n][:, c * PACK : (c + 1) * PACK, :]
-            if c * N_TILES + n >= 5:
-                nc.vector.tensor_copy(out=by_column_grouped(gt_grouped[:]), in_=by_column(rows))
-            else:
-                nc.scalar.copy(out=by_column_grouped(gt_grouped[:]), in_=by_column(rows))
+            for s in range(len(streams)):
+                if first_cols[s] // N_TILE != n:
+                    continue
+                first = first_cols[s] % N_TILE
+                columns = by_column_grouped(gt_grouped[:, first : first + widths[s], :])
+                rows = by_column(stream_sb[s][:, c * PACK : (c + 1) * PACK, :])
+                if c * N_TILES + n >= 5:
+                    nc.vector.tensor_copy(out=columns, in_=rows)
+                else:
+                    nc.scalar.copy(out=columns, in_=rows)
             nc.vector.quantize_mx(
                 out=gt_codes[:, c, n, :].bitcast(E4M3_X4),
                 scales=gt_scales[:, c, n, :],
                 in_=gt_grouped[:].rearrange("p w t -> p (w t)"),
             )
+
+        si, tg, sf, so, tg2 = [
+            [resident.tile([P, ROWS, M_TILE], F32, name="%s%d" % (name, hb)) for hb in range(H_BLOCKS)]
+            for name in ("si", "tg", "sf", "so", "tg2")
+        ]
+
+        def gate_activations(hb, c):
+            rows = slice(c * PACK, (c + 1) * PACK)
+            cols = slice(hb * M_TILE, (hb + 1) * M_TILE)
+            nc.scalar.activation(out=si[hb][:, rows, :], in_=gf_sb[GATE_I][:, rows, cols], func=FUNC.Sigmoid)
+            nc.scalar.activation(out=tg[hb][:, rows, :], in_=gf_sb[GATE_G][:, rows, cols], func=FUNC.Tanh)
+            nc.scalar.activation(out=sf[hb][:, rows, :], in_=gf_sb[GATE_F][:, rows, cols], func=FUNC.Sigmoid)
+            nc.scalar.activation(out=tg2[hb][:, rows, :], in_=tg[hb][:, rows, :], func=FUNC.Square)
+            nc.scalar.activation(out=so[hb][:, rows, :], in_=gf_sb[GATE_O][:, rows, cols], func=FUNC.Sigmoid)
 
         def gate_gradients(hb, first_pass, n_passes):
             rows = slice(first_pass * PACK, (first_pass + n_passes) * PACK)
@@ -158,30 +177,24 @@ def tile_dependency_pa_v_kernel(
                     in_=dg_grouped[:].rearrange("p c m t -> p (c m t)"),
                 )
 
-            si = activation("si", FUNC.Sigmoid, gf_sb[GATE_I][:, rows, cols])
-            tg = activation("tg", FUNC.Tanh, gf_sb[GATE_G][:, rows, cols])
-            sf = activation("sf", FUNC.Sigmoid, gf_sb[GATE_F][:, rows, cols])
-            tg2 = activation("tg2", FUNC.Square, tg[:])
-            so = activation("so", FUNC.Sigmoid, gf_sb[GATE_O][:, rows, cols])
-
-            input_part = product("input_part", si[:], tg[:])
-            forget_part = product("forget_part", sf[:], cell_sb[:, rows, cols])
-            minus_i = minus_one_times("minus_i", si[:], input_part[:])
+            input_part = product("input_part", si[hb][:, rows, :], tg[hb][:, rows, :])
+            forget_part = product("forget_part", sf[hb][:, rows, :], cell_sb[:, rows, cols])
+            minus_i = minus_one_times("minus_i", si[hb][:, rows, :], input_part[:])
             c2 = chain.tile(shape, F32, name="c2")
             nc.vector.tensor_tensor(out=c2[:], in0=input_part[:], in1=forget_part[:], op=ALU.add)
             minus_tc = activation("minus_tc", FUNC.Tanh, c2[:], scale=-1.0)
             tc2 = activation("tc2", FUNC.Square, minus_tc[:])
 
-            go_so = product("go_so", so[:], go_sb[:, rows, cols])
-            minus_do_tc = minus_one_times("minus_do_tc", so[:], go_so[:])
+            go_so = product("go_so", so[hb][:, rows, :], go_sb[:, rows, cols])
+            minus_do_tc = minus_one_times("minus_do_tc", so[hb][:, rows, :], go_so[:])
             do_grouped = finish(GATE_O, minus_do_tc, minus_tc)
             minus_dc2 = minus_one_times("minus_dc2", tc2[:], go_so[:])
             quantise_dg(GATE_O, do_grouped)
             di_grouped = finish(GATE_I, minus_i, minus_dc2)
-            minus_f = minus_one_times("minus_f", sf[:], forget_part[:])
+            minus_f = minus_one_times("minus_f", sf[hb][:, rows, :], forget_part[:])
             quantise_dg(GATE_I, di_grouped)
             df_grouped = finish(GATE_F, minus_f, minus_dc2)
-            minus_g = minus_one_times("minus_g", tg2[:], si[:])
+            minus_g = minus_one_times("minus_g", tg2[hb][:, rows, :], si[hb][:, rows, :])
             quantise_dg(GATE_F, df_grouped)
             dgg_grouped = finish(GATE_G, minus_g, minus_dc2)
             quantise_dg(GATE_G, dgg_grouped)
@@ -211,8 +224,11 @@ def tile_dependency_pa_v_kernel(
 
         gates_as_they_finish = (GATE_O, GATE_I, GATE_F, GATE_G)
 
-        gate_gradients(0, 0, 1)
-        gate_gradients(0, 1, 1)
+        for c in range(PASSES):
+            gate_activations(0, c)
+            gate_gradients(0, c, 1)
+        for c in range(PASSES):
+            gate_activations(1, c)
         for c in range(PASSES):
             for n in range(N_TILES):
                 quantise_gt(c, n)

@@ -1,4 +1,5 @@
 import concourse.mybir as mybir
+from concourse.masks import make_identity
 
 F32 = mybir.dt.float32
 BF16 = mybir.dt.bfloat16
@@ -22,6 +23,7 @@ M_TILE = 128
 H_BLOCKS = H // M_TILE
 N_TILE = 512
 N_TILES = 3
+FIRST_TILE_ON_VECTOR = 5
 RUN = 4
 
 FLOPS = 2 * TOKENS * (GATES * H) * (N_TILES * N_TILE)
@@ -103,6 +105,9 @@ def tile_dependency_pa_v_kernel(
         dg_codes = resident.tile([P, H_BLOCKS, GATES, PASSES, M_TILE], U32, name="dg_codes", align_bytes=64)
         dg_scales = resident.tile([P, H_BLOCKS, GATES, PASSES, M_TILE], U8, name="dg_scales", align_bytes=64)
 
+        identity = resident.tile([P, P], F32, name="identity")
+        make_identity(nc, identity[:])
+
         def quantise_gt(c, n):
             gt_grouped = gt_grouped_pool.tile([P, N_TILE, PACK], BF16, name="gt_grouped", align_bytes=64)
             for s in range(len(streams)):
@@ -111,7 +116,7 @@ def tile_dependency_pa_v_kernel(
                 first = first_cols[s] % N_TILE
                 columns = by_column_grouped(gt_grouped[:, first : first + widths[s], :])
                 rows = by_column(stream_sb[s][:, c * PACK : (c + 1) * PACK, :])
-                if c * N_TILES + n >= 5:
+                if c * N_TILES + n >= FIRST_TILE_ON_VECTOR:
                     nc.vector.tensor_copy(out=columns, in_=rows)
                 else:
                     nc.scalar.copy(out=columns, in_=rows)
@@ -180,9 +185,17 @@ def tile_dependency_pa_v_kernel(
             input_part = product("input_part", si[hb][:, rows, :], tg[hb][:, rows, :])
             forget_part = product("forget_part", sf[hb][:, rows, :], cell_sb[:, rows, cols])
             minus_i = minus_one_times("minus_i", si[hb][:, rows, :], input_part[:])
-            c2 = chain.tile(shape, F32, name="c2")
-            nc.vector.tensor_tensor(out=c2[:], in0=input_part[:], in1=forget_part[:], op=ALU.add)
-            minus_tc = activation("minus_tc", FUNC.Tanh, c2[:], scale=-1.0)
+            minus_tc = gates.tile(shape, F32, name="minus_tc")
+            if hb == 0:
+                c2_sb = chain.tile(shape, F32, name="c2")
+                nc.vector.tensor_tensor(out=c2_sb[:], in0=input_part[:], in1=forget_part[:], op=ALU.add)
+                nc.scalar.activation(out=minus_tc[:], in_=c2_sb[:], func=FUNC.Tanh, scale=-1.0)
+            for k in range(n_passes if hb == 1 else 0):
+                k_rows = slice(k * PACK, (k + 1) * PACK)
+                c2 = psum.tile([P, PACK, M_TILE], F32, name="acc")
+                nc.tensor.matmul(out=c2[:], lhsT=identity[:], rhs=input_part[:, k_rows, :], start=True, stop=False)
+                nc.tensor.matmul(out=c2[:], lhsT=identity[:], rhs=forget_part[:, k_rows, :], start=False, stop=True)
+                nc.scalar.activation(out=minus_tc[:, k_rows, :], in_=c2[:], func=FUNC.Tanh, scale=-1.0)
             tc2 = activation("tc2", FUNC.Square, minus_tc[:])
 
             go_so = product("go_so", so[hb][:, rows, :], go_sb[:, rows, cols])

@@ -16,14 +16,15 @@ K_PASS = P * PACK
 TOKENS = 1024
 PASSES = TOKENS // K_PASS
 ROWS = PASSES * PACK
+PIECE = 2
 H = 256
 GATE_I, GATE_F, GATE_G, GATE_O = 0, 1, 2, 3
 GATES = 4
+FINISH_ORDER = (GATE_O, GATE_I, GATE_F, GATE_G)
 M_TILE = 128
 H_BLOCKS = H // M_TILE
 N_TILE = 512
 N_TILES = 3
-FIRST_TILE_ON_VECTOR = 5
 RUN = 4
 
 FLOPS = 2 * TOKENS * (GATES * H) * (N_TILES * N_TILE)
@@ -67,14 +68,15 @@ def tile_dependency_pa_v_kernel(
     nc = tc.nc
     with (
         tc.tile_pool(name="resident", bufs=1) as resident,
-        tc.tile_pool(name="gates", bufs=2) as gates,
-        tc.tile_pool(name="chain", bufs=1) as chain,
-        tc.tile_pool(name="grouped", bufs=2) as grouped_pool,
-        tc.tile_pool(name="gt_grouped", bufs=3) as gt_grouped_pool,
+        tc.tile_pool(name="gt_grouped", bufs=4) as gt_grouped_pool,
         tc.tile_pool(name="stage", bufs=8) as stage,
         tc.psum_pool(name="psum", bufs=8) as psum,
+        tc.manual_schedule(),
     ):
-        gf_sb = [resident.tile([P, ROWS, H], F32, name="gf_sb%d" % g) for g in range(GATES)]
+        identity = resident.tile([P, P], F32, name="identity")
+        make_identity(nc, identity[:])
+
+        gf_sb = resident.tile([P, ROWS, GATES * H], F32, name="gf_sb")
         cell_sb = resident.tile([P, ROWS, H], BF16, name="cell_sb")
         go_sb = resident.tile([P, ROWS, H], BF16, name="go_sb")
         streams = (hn_chunks, hn_tags, x, tags, chunks)
@@ -82,170 +84,260 @@ def tile_dependency_pa_v_kernel(
         first_cols = [sum(widths[:s]) for s in range(len(streams))]
         stream_sb = [resident.tile([P, ROWS, widths[s]], BF16, name="stream_sb%d" % s) for s in range(len(streams))]
 
-        def load(dst, c, dst_cols, src):
-            nc.sync.dma_start(
-                out=dst[:, c * PACK : (c + 1) * PACK, dst_cols],
-                in_=src[c * K_PASS : (c + 1) * K_PASS, :].rearrange("(p j) w -> p j w", j=PACK),
-            )
+        def streams_of(n):
+            return [s for s in range(len(streams)) if first_cols[s] // N_TILE == n]
 
-        whole_gate = slice(0, H)
-        for c in range(PASSES):
-            load(gf_sb[GATE_I], c, whole_gate, gf[:, GATE_I * H : (GATE_I + 1) * H])
-            load(gf_sb[GATE_G], c, whole_gate, gf[:, GATE_G * H : (GATE_G + 1) * H])
-            load(gf_sb[GATE_F], c, whole_gate, gf[:, GATE_F * H : (GATE_F + 1) * H])
-            load(cell_sb, c, whole_gate, c0[0, :, :])
-            load(gf_sb[GATE_O], c, whole_gate, gf[:, GATE_O * H : (GATE_O + 1) * H])
-            load(go_sb, c, whole_gate, grad_out[:, 0:H])
-        for c in range(PASSES):
-            for s in range(len(streams)):
-                load(stream_sb[s], c, slice(0, widths[s]), streams[s])
+        def load(dst, src, c, first=0, n_rows=PACK):
+            nc.sync.dma_start(
+                out=dst[:, c * PACK + first : c * PACK + first + n_rows, :],
+                in_=src[c * K_PASS : (c + 1) * K_PASS, :].rearrange("(p j) w -> p j w", j=PACK)[
+                    :, first : first + n_rows, :
+                ],
+            )
 
         gt_codes = resident.tile([P, PASSES, N_TILES, N_TILE], U32, name="gt_codes", align_bytes=64)
         gt_scales = resident.tile([P, PASSES, N_TILES, N_TILE], U8, name="gt_scales", align_bytes=64)
-        dg_codes = resident.tile([P, H_BLOCKS, GATES, PASSES, M_TILE], U32, name="dg_codes", align_bytes=64)
-        dg_scales = resident.tile([P, H_BLOCKS, GATES, PASSES, M_TILE], U8, name="dg_scales", align_bytes=64)
+        dg_codes = resident.tile([P, H_BLOCKS, PASSES, GATES, M_TILE], U32, name="dg_codes", align_bytes=64)
+        dg_scales = resident.tile([P, H_BLOCKS, PASSES, GATES, M_TILE], U8, name="dg_scales", align_bytes=64)
 
-        identity = resident.tile([P, P], F32, name="identity")
-        make_identity(nc, identity[:])
+        def new_gt_grouped():
+            return gt_grouped_pool.tile([P, N_TILE, PACK], BF16, name="gt_grouped", align_bytes=64)
 
-        def quantise_gt(c, n):
-            gt_grouped = gt_grouped_pool.tile([P, N_TILE, PACK], BF16, name="gt_grouped", align_bytes=64)
-            for s in range(len(streams)):
-                if first_cols[s] // N_TILE != n:
-                    continue
-                first = first_cols[s] % N_TILE
-                columns = by_column_grouped(gt_grouped[:, first : first + widths[s], :])
-                rows = by_column(stream_sb[s][:, c * PACK : (c + 1) * PACK, :])
-                if c * N_TILES + n >= FIRST_TILE_ON_VECTOR:
-                    nc.vector.tensor_copy(out=columns, in_=rows)
-                else:
-                    nc.scalar.copy(out=columns, in_=rows)
+        def regroup_gt(copy, gt_grouped, c, s, first, width):
+            at = first_cols[s] % N_TILE + first
+            copy(
+                out=by_column_grouped(gt_grouped[:, at : at + width, :]),
+                in_=by_column(stream_sb[s][:, c * PACK : (c + 1) * PACK, first : first + width]),
+            )
+
+        def regroup_tile(copy, c, n):
+            gt_grouped = new_gt_grouped()
+            for s in streams_of(n):
+                regroup_gt(copy, gt_grouped, c, s, 0, widths[s])
+            return gt_grouped
+
+        def quantise_gt(c, n, gt_grouped):
             nc.vector.quantize_mx(
                 out=gt_codes[:, c, n, :].bitcast(E4M3_X4),
                 scales=gt_scales[:, c, n, :],
                 in_=gt_grouped[:].rearrange("p w t -> p (w t)"),
             )
 
-        si, tg, sf, so, tg2 = [
-            [resident.tile([P, ROWS, M_TILE], F32, name="%s%d" % (name, hb)) for hb in range(H_BLOCKS)]
-            for name in ("si", "tg", "sf", "so", "tg2")
+        si, sf, tg, so = [gf_sb[:, :, g * H : (g + 1) * H] for g in (GATE_I, GATE_F, GATE_G, GATE_O)]
+        names = ("minus_g", "ip", "fp", "minus_i", "minus_f", "go_so", "minus_do_tc", "minus_tc", "minus_dc2")
+        minus_g, ip, fp, minus_i, minus_f, go_so, minus_do_tc, minus_tc, minus_dc2 = [
+            resident.tile([P, ROWS, H], F32, name=name) for name in names
         ]
+        c2_sb = resident.tile([P, ROWS, M_TILE], F32, name="c2_sb")
+        dg_grouped = resident.tile(
+            [P, H_BLOCKS, PASSES, GATES, M_TILE, PACK], BF16, name="dg_grouped", align_bytes=64
+        )
 
-        def gate_activations(hb, c):
-            rows = slice(c * PACK, (c + 1) * PACK)
-            cols = slice(hb * M_TILE, (hb + 1) * M_TILE)
-            nc.scalar.activation(out=si[hb][:, rows, :], in_=gf_sb[GATE_I][:, rows, cols], func=FUNC.Sigmoid)
-            nc.scalar.activation(out=tg[hb][:, rows, :], in_=gf_sb[GATE_G][:, rows, cols], func=FUNC.Tanh)
-            nc.scalar.activation(out=sf[hb][:, rows, :], in_=gf_sb[GATE_F][:, rows, cols], func=FUNC.Sigmoid)
-            nc.scalar.activation(out=tg2[hb][:, rows, :], in_=tg[hb][:, rows, :], func=FUNC.Square)
-            nc.scalar.activation(out=so[hb][:, rows, :], in_=gf_sb[GATE_O][:, rows, cols], func=FUNC.Sigmoid)
+        def cols_of(hb):
+            return slice(hb * M_TILE, (hb + 1) * M_TILE)
 
-        def gate_gradients(hb, first_pass, n_passes):
-            rows = slice(first_pass * PACK, (first_pass + n_passes) * PACK)
-            cols = slice(hb * M_TILE, (hb + 1) * M_TILE)
-            shape = [P, n_passes * PACK, M_TILE]
+        def gate_activations(hb, r):
+            cols = cols_of(hb)
+            for gate, func in ((si, FUNC.Sigmoid), (tg, FUNC.Tanh), (sf, FUNC.Sigmoid)):
+                nc.scalar.activation(out=gate[:, r, cols], in_=gate[:, r, cols], func=func)
+            nc.scalar.activation(out=minus_g[:, r, cols], in_=tg[:, r, cols], func=FUNC.Square)
+            nc.scalar.activation(out=so[:, r, cols], in_=so[:, r, cols], func=FUNC.Sigmoid)
 
-            def activation(name, func, in_, scale=1.0):
-                result = gates.tile(shape, F32, name=name)
-                nc.scalar.activation(out=result[:], in_=in_, func=func, scale=scale)
-                return result
+        def product(out, in0, in1, hb, r):
+            cols = cols_of(hb)
+            nc.vector.tensor_tensor(out=out[:, r, cols], in0=in0[:, r, cols], in1=in1[:, r, cols], op=ALU.mult)
 
-            def product(name, in0, in1):
-                result = chain.tile(shape, F32, name=name)
-                nc.vector.tensor_tensor(out=result[:], in0=in0, in1=in1, op=ALU.mult)
-                return result
+        def minus_one_times(out, in0, in1, hb, r):
+            cols = cols_of(hb)
+            nc.vector.scalar_tensor_tensor(
+                out=out[:, r, cols], in0=in0[:, r, cols], scalar=1.0, in1=in1[:, r, cols],
+                op0=ALU.subtract, op1=ALU.mult,
+            )
 
-            def minus_one_times(name, in0, in1):
-                result = chain.tile(shape, F32, name=name)
-                nc.vector.scalar_tensor_tensor(
-                    out=result[:], in0=in0, scalar=1.0, in1=in1, op0=ALU.subtract, op1=ALU.mult
-                )
-                return result
+        def cell_sum(r):
+            cols = cols_of(0)
+            nc.vector.tensor_tensor(out=c2_sb[:, r, :], in0=ip[:, r, cols], in1=fp[:, r, cols], op=ALU.add)
 
-            def finish(g, in0, in1):
-                dg_grouped = grouped_pool.tile([P, n_passes, M_TILE, PACK], BF16, name="dg_grouped%d" % g, align_bytes=64)
-                for k in range(n_passes):
-                    k_rows = slice(k * PACK, (k + 1) * PACK)
-                    nc.vector.tensor_tensor(
-                        out=by_column_grouped(dg_grouped[:, k, :, :]),
-                        in0=by_column(in0[:, k_rows, :]),
-                        in1=by_column(in1[:, k_rows, :]),
-                        op=ALU.mult,
-                    )
-                return dg_grouped
+        def cell_tanh(hb, r, c2):
+            cols = cols_of(hb)
+            nc.scalar.activation(out=minus_tc[:, r, cols], in_=c2, func=FUNC.Tanh, scale=-1.0)
+            nc.scalar.activation(out=minus_dc2[:, r, cols], in_=minus_tc[:, r, cols], func=FUNC.Square)
 
-            def quantise_dg(g, dg_grouped):
-                passes = slice(first_pass, first_pass + n_passes)
-                nc.vector.quantize_mx(
-                    out=dg_codes[:, hb, g, passes, :].rearrange("p c m -> p (c m)").bitcast(E5M2_X4),
-                    scales=dg_scales[:, hb, g, passes, :].rearrange("p c m -> p (c m)"),
-                    in_=dg_grouped[:].rearrange("p c m t -> p (c m t)"),
-                )
+        last_product = {
+            GATE_O: (minus_do_tc, minus_tc),
+            GATE_I: (minus_i, minus_dc2),
+            GATE_F: (minus_f, minus_dc2),
+            GATE_G: (minus_g, minus_dc2),
+        }
 
-            input_part = product("input_part", si[hb][:, rows, :], tg[hb][:, rows, :])
-            forget_part = product("forget_part", sf[hb][:, rows, :], cell_sb[:, rows, cols])
-            minus_i = minus_one_times("minus_i", si[hb][:, rows, :], input_part[:])
-            minus_tc = gates.tile(shape, F32, name="minus_tc")
-            if hb == 0:
-                c2_sb = chain.tile(shape, F32, name="c2")
-                nc.vector.tensor_tensor(out=c2_sb[:], in0=input_part[:], in1=forget_part[:], op=ALU.add)
-                nc.scalar.activation(out=minus_tc[:], in_=c2_sb[:], func=FUNC.Tanh, scale=-1.0)
-            for k in range(n_passes if hb == 1 else 0):
-                k_rows = slice(k * PACK, (k + 1) * PACK)
-                c2 = psum.tile([P, PACK, M_TILE], F32, name="acc")
-                nc.tensor.matmul(out=c2[:], lhsT=identity[:], rhs=input_part[:, k_rows, :], start=True, stop=False)
-                nc.tensor.matmul(out=c2[:], lhsT=identity[:], rhs=forget_part[:, k_rows, :], start=False, stop=True)
-                nc.scalar.activation(out=minus_tc[:, k_rows, :], in_=c2[:], func=FUNC.Tanh, scale=-1.0)
-            tc2 = activation("tc2", FUNC.Square, minus_tc[:])
+        def finish(hb, g, c):
+            in0, in1 = last_product[g]
+            r = slice(c * PACK, (c + 1) * PACK)
+            nc.vector.tensor_tensor(
+                out=by_column_grouped(dg_grouped[:, hb, c, g, :, :]),
+                in0=by_column(in0[:, r, cols_of(hb)]),
+                in1=by_column(in1[:, r, cols_of(hb)]),
+                op=ALU.mult,
+            )
 
-            go_so = product("go_so", so[hb][:, rows, :], go_sb[:, rows, cols])
-            minus_do_tc = minus_one_times("minus_do_tc", so[hb][:, rows, :], go_so[:])
-            do_grouped = finish(GATE_O, minus_do_tc, minus_tc)
-            minus_dc2 = minus_one_times("minus_dc2", tc2[:], go_so[:])
-            quantise_dg(GATE_O, do_grouped)
-            di_grouped = finish(GATE_I, minus_i, minus_dc2)
-            minus_f = minus_one_times("minus_f", sf[hb][:, rows, :], forget_part[:])
-            quantise_dg(GATE_I, di_grouped)
-            df_grouped = finish(GATE_F, minus_f, minus_dc2)
-            minus_g = minus_one_times("minus_g", tg2[hb][:, rows, :], si[hb][:, rows, :])
-            quantise_dg(GATE_F, df_grouped)
-            dgg_grouped = finish(GATE_G, minus_g, minus_dc2)
-            quantise_dg(GATE_G, dgg_grouped)
+        def quantise_dg(hb, c, gates):
+            nc.vector.quantize_mx(
+                out=dg_codes[:, hb, c, gates, :].rearrange("p g m -> p (g m)").bitcast(E5M2_X4),
+                scales=dg_scales[:, hb, c, gates, :].rearrange("p g m -> p (g m)"),
+                in_=dg_grouped[:, hb, c, gates, :, :].rearrange("p g m t -> p (g m t)"),
+            )
 
-        def multiply_and_store(hb, g):
+        def new_acc():
+            return psum.tile([M_TILE, N_TILE], F32, name="acc")
+
+        def multiply(acc, hb, g, n, c):
+            nc.tensor.matmul_mx(
+                out=acc[:],
+                lhsT=dg_codes[:, hb, c, g, :].bitcast(E5M2_X4),
+                lhsT_scale=dg_scales[:, hb, c, g, :],
+                rhs=gt_codes[:, c, n, :].bitcast(E4M3_X4),
+                rhs_scale=gt_scales[:, c, n, :],
+                start=(c == 0),
+                stop=(c == PASSES - 1),
+            )
+
+        def store(copy, acc, hb, g, n):
             first_row = g * H + hb * M_TILE
-            for n in range(N_TILES):
-                acc = psum.tile([M_TILE, N_TILE], F32, name="acc")
-                for c in range(PASSES):
-                    nc.tensor.matmul_mx(
-                        out=acc[:],
-                        lhsT=dg_codes[:, hb, g, c, :].bitcast(E5M2_X4),
-                        lhsT_scale=dg_scales[:, hb, g, c, :],
-                        rhs=gt_codes[:, c, n, :].bitcast(E4M3_X4),
-                        rhs_scale=gt_scales[:, c, n, :],
-                        start=(c == 0),
-                        stop=(c == PASSES - 1),
-                    )
-                result = stage.tile([M_TILE, N_TILE], F32, name="result")
-                if hb == H_BLOCKS - 1 and g == gates_as_they_finish[-1]:
-                    nc.vector.tensor_copy(out=result[:], in_=acc[:])
-                else:
-                    nc.scalar.copy(out=result[:], in_=acc[:])
-                nc.sync.dma_start(
-                    out=out[first_row : first_row + M_TILE, n * N_TILE : (n + 1) * N_TILE], in_=result[:]
-                )
+            result = stage.tile([M_TILE, N_TILE], F32, name="result")
+            copy(out=result[:], in_=acc[:])
+            nc.sync.dma_start(out=out[first_row : first_row + M_TILE, n * N_TILE : (n + 1) * N_TILE], in_=result[:])
 
-        gates_as_they_finish = (GATE_O, GATE_I, GATE_F, GATE_G)
+        def products_of(hb, g, n):
+            acc = new_acc()
+            for c in range(PASSES):
+                multiply(acc, hb, g, n, c)
+            return acc
 
+        rows = [slice(first, first + PIECE) for first in range(0, ROWS, PIECE)]
+        by_pass = [slice(c * PACK, (c + 1) * PACK) for c in range(PASSES)]
+        act = nc.scalar.copy
+        vec = nc.vector.tensor_copy
+
+        def input_parts(hb, r):
+            product(ip, si, tg, hb, r)
+            minus_one_times(minus_g, minus_g, si, hb, r)
+            minus_one_times(minus_i, si, ip, hb, r)
+
+        def output_parts(hb, r):
+            product(go_so, so, go_sb, hb, r)
+            minus_one_times(minus_do_tc, so, go_so, hb, r)
+
+        def load_gt(c, n):
+            for s in streams_of(n):
+                load(stream_sb[s], streams[s], c)
+
+        load(gf_sb, gf, 0, 0, PIECE)
+        load(cell_sb, c0[0, :, :], 0)
+        load(gf_sb, gf, 0, PIECE, PIECE)
+        load(go_sb, grad_out[:, 0:H], 0)
+        load(gf_sb, gf, 1, 0, PIECE)
+        load(cell_sb, c0[0, :, :], 1)
+        load(gf_sb, gf, 1, PIECE, PIECE)
+        load_gt(0, 0)
+        load(go_sb, grad_out[:, 0:H], 1)
+        load_gt(1, 0)
+        for n in (1, 2):
+            for c in range(PASSES):
+                load_gt(c, n)
+
+        gate_activations(0, rows[0])
+        gate_activations(1, rows[0])
+        input_parts(0, rows[0])
+        product(fp, sf, cell_sb, 0, rows[0])
+        input_parts(1, rows[0])
+        minus_one_times(minus_f, sf, fp, 0, rows[0])
+        product(fp, sf, cell_sb, 1, rows[0])
+        cell_sum(rows[0])
+        minus_one_times(minus_f, sf, fp, 1, rows[0])
+        gate_activations(0, rows[1])
+        input_parts(0, rows[1])
+        product(fp, sf, cell_sb, 0, rows[1])
+        output_parts(0, rows[0])
+        cell_sum(rows[1])
+        minus_one_times(minus_f, sf, fp, 0, rows[1])
+        output_parts(0, rows[1])
+        gate_activations(1, rows[1])
+        cell_tanh(0, by_pass[0], c2_sb[:, by_pass[0], :])
+        finish(0, GATE_O, 0)
+        minus_one_times(minus_dc2, minus_dc2, go_so, 0, by_pass[0])
+        gate_activations(0, rows[2])
+        product(ip, si, tg, 0, rows[2])
+        for g in FINISH_ORDER[1:]:
+            finish(0, g, 0)
+        gate_activations(1, rows[2])
+        gate_activations(0, rows[3])
+        gate_activations(1, rows[3])
+        product(fp, sf, cell_sb, 0, rows[2])
+        quantise_dg(0, 0, slice(0, GATES))
+        product(ip, si, tg, 0, rows[3])
+        product(fp, sf, cell_sb, 0, rows[3])
+        cell_sum(by_pass[1])
+        g00 = new_gt_grouped()
+        regroup_gt(act, g00, 0, 0, 0, H)
+        cell_tanh(0, by_pass[1], c2_sb[:, by_pass[1], :])
+        regroup_gt(act, g00, 0, 0, H, H)
+        minus_one_times(minus_i, si, ip, 0, by_pass[1])
+        minus_one_times(minus_f, sf, fp, 0, by_pass[1])
+        product(go_so, so, go_sb, 0, by_pass[1])
+        minus_one_times(minus_g, minus_g, si, 0, by_pass[1])
+        minus_one_times(minus_do_tc, so, go_so, 0, by_pass[1])
+        minus_one_times(minus_dc2, minus_dc2, go_so, 0, by_pass[1])
+        for g in FINISH_ORDER:
+            finish(0, g, 1)
+
+        quantise_gt(0, 0, g00)
+        rest = slice(PIECE, ROWS)
+        product(ip, si, tg, 1, rest)
+        quantise_dg(0, 1, slice(0, GATES))
+        g10 = regroup_tile(act, 1, 0)
+        product(fp, sf, cell_sb, 1, rest)
+        quantise_gt(1, 0, g10)
+        acc0 = [products_of(0, g, 0) for g in FINISH_ORDER]
+        c2_acc = []
         for c in range(PASSES):
-            gate_activations(0, c)
-            gate_gradients(0, c, 1)
+            c2 = psum.tile([P, PACK, M_TILE], F32, name="acc")
+            k = by_pass[c]
+            nc.tensor.matmul(out=c2[:], lhsT=identity[:], rhs=ip[:, k, cols_of(1)], start=True, stop=False)
+            nc.tensor.matmul(out=c2[:], lhsT=identity[:], rhs=fp[:, k, cols_of(1)], start=False, stop=True)
+            c2_acc.append(c2)
+        g01 = regroup_tile(act, 0, 1)
+        minus_one_times(minus_i, si, ip, 1, rest)
+        for g, acc in zip(FINISH_ORDER, acc0):
+            store(act, acc, 0, g, 0)
+        minus_one_times(minus_f, sf, fp, 1, rest)
+        quantise_gt(0, 1, g01)
+        g02 = regroup_tile(vec, 0, 2)
+        product(go_so, so, go_sb, 1, slice(0, ROWS))
+        g11 = regroup_tile(act, 1, 1)
         for c in range(PASSES):
-            gate_activations(1, c)
-        for c in range(PASSES):
+            cell_tanh(1, by_pass[c], c2_acc[c][:])
+        quantise_gt(0, 2, g02)
+        quantise_gt(1, 1, g11)
+        acc1 = [products_of(0, g, 1) for g in FINISH_ORDER]
+        g12 = regroup_tile(vec, 1, 2)
+        for g, acc in zip(FINISH_ORDER, acc1):
+            store(act, acc, 0, g, 1)
+        minus_one_times(minus_do_tc, so, go_so, 1, slice(0, ROWS))
+        quantise_gt(1, 2, g12)
+        acc2 = [products_of(0, g, 2) for g in FINISH_ORDER]
+        for g, acc in zip(FINISH_ORDER, acc2):
+            store(act, acc, 0, g, 2)
+        for g in FINISH_ORDER:
+            last = g == FINISH_ORDER[-1]
+            accs = [new_acc() for n in range(N_TILES)]
+            for c in range(PASSES):
+                finish(1, g, c)
+                if g == GATE_O and c == 0:
+                    minus_one_times(minus_dc2, minus_dc2, go_so, 1, slice(0, ROWS))
+                if g == GATE_F and c == 0:
+                    minus_one_times(minus_g, minus_g, si, 1, rest)
+                quantise_dg(1, c, slice(g, g + 1))
+                for n in range(N_TILES):
+                    multiply(accs[n], 1, g, n, c)
             for n in range(N_TILES):
-                quantise_gt(c, n)
-        gate_gradients(1, 0, PASSES)
-        for hb in range(H_BLOCKS):
-            for g in gates_as_they_finish:
-                multiply_and_store(hb, g)
+                store(vec if last and n != 1 else act, accs[n], 1, g, n)

@@ -123,45 +123,78 @@ def tile_dependency_pa_v_kernel(
                 in_=gt_grouped[:].rearrange("p w t -> p (w t)"),
             )
 
-        si, sf, tg, so = [gf_sb[:, :, g * H : (g + 1) * H] for g in (GATE_I, GATE_F, GATE_G, GATE_O)]
-        names = ("minus_g", "ip", "fp", "minus_i", "minus_f", "go_so", "minus_do_tc", "minus_tc", "minus_dc2")
-        minus_g, ip, fp, minus_i, minus_f, go_so, minus_do_tc, minus_tc, minus_dc2 = [
-            resident.tile([P, ROWS, H], F32, name=name) for name in names
+        names = ("si", "tg", "sf", "so", "tg2", "ip", "fp", "go_so", "minus_tc", "tc2")
+        si, tg, sf, so, tg2, ip, fp, go_so, minus_tc, tc2 = [
+            resident.tile([P, H_BLOCKS, ROWS, M_TILE], F32, name=name) for name in names
         ]
+        minus_i, minus_f, minus_g, minus_do_tc, minus_dc2 = tg, sf, tg2, so, tc2
         c2_sb = resident.tile([P, ROWS, M_TILE], F32, name="c2_sb")
         dg_grouped = resident.tile(
             [P, H_BLOCKS, PASSES, GATES, M_TILE, PACK], BF16, name="dg_grouped", align_bytes=64
         )
 
-        def cols_of(hb):
-            return slice(hb * M_TILE, (hb + 1) * M_TILE)
+        def part(t, hb, r):
+            return t[:, :, r, :] if hb is None else t[:, hb, r, :]
+
+        def part_of_rows(t, hb, r, first=0):
+            if hb is None:
+                return t[:, r, first : first + H].rearrange("p r (b m) -> p b r m", m=M_TILE)
+            return t[:, r, first + hb * M_TILE : first + (hb + 1) * M_TILE]
+
+        def activate(out_tile, gate, func, hb, r):
+            nc.scalar.activation(out=part(out_tile, hb, r), in_=part_of_rows(gf_sb, hb, r, gate * H), func=func)
+
+        def square(out_tile, in_tile, hb, r):
+            nc.scalar.activation(out=part(out_tile, hb, r), in_=part(in_tile, hb, r), func=FUNC.Square)
 
         def gate_activations(hb, r):
-            cols = cols_of(hb)
-            for gate, func in ((si, FUNC.Sigmoid), (tg, FUNC.Tanh), (sf, FUNC.Sigmoid)):
-                nc.scalar.activation(out=gate[:, r, cols], in_=gate[:, r, cols], func=func)
-            nc.scalar.activation(out=minus_g[:, r, cols], in_=tg[:, r, cols], func=FUNC.Square)
-            nc.scalar.activation(out=so[:, r, cols], in_=so[:, r, cols], func=FUNC.Sigmoid)
+            activate(si, GATE_I, FUNC.Sigmoid, hb, r)
+            activate(tg, GATE_G, FUNC.Tanh, hb, r)
+            activate(sf, GATE_F, FUNC.Sigmoid, hb, r)
+            square(tg2, tg, hb, r)
+            activate(so, GATE_O, FUNC.Sigmoid, hb, r)
 
-        def product(out, in0, in1, hb, r):
-            cols = cols_of(hb)
-            nc.vector.tensor_tensor(out=out[:, r, cols], in0=in0[:, r, cols], in1=in1[:, r, cols], op=ALU.mult)
+        def product(out, in0, in1):
+            nc.vector.tensor_tensor(out=out, in0=in0, in1=in1, op=ALU.mult)
 
-        def minus_one_times(out, in0, in1, hb, r):
-            cols = cols_of(hb)
-            nc.vector.scalar_tensor_tensor(
-                out=out[:, r, cols], in0=in0[:, r, cols], scalar=1.0, in1=in1[:, r, cols],
-                op0=ALU.subtract, op1=ALU.mult,
-            )
+        def minus_one_times(out, in0, in1):
+            nc.vector.scalar_tensor_tensor(out=out, in0=in0, scalar=1.0, in1=in1, op0=ALU.subtract, op1=ALU.mult)
+
+        def make_ip(hb, r):
+            product(part(ip, hb, r), part(si, hb, r), part(tg, hb, r))
+
+        def make_fp(hb, r):
+            product(part(fp, hb, r), part(sf, hb, r), part_of_rows(cell_sb, hb, r))
+
+        def make_go_so(hb, r):
+            product(part(go_so, hb, r), part(so, hb, r), part_of_rows(go_sb, hb, r))
+
+        def make_minus_i(hb, r):
+            minus_one_times(part(minus_i, hb, r), part(si, hb, r), part(ip, hb, r))
+
+        def make_minus_f(hb, r):
+            minus_one_times(part(minus_f, hb, r), part(sf, hb, r), part(fp, hb, r))
+
+        def make_minus_g(hb, r):
+            minus_one_times(part(minus_g, hb, r), part(tg2, hb, r), part(si, hb, r))
+
+        def make_minus_do_tc(hb, r):
+            minus_one_times(part(minus_do_tc, hb, r), part(so, hb, r), part(go_so, hb, r))
+
+        def make_minus_dc2(hb, r):
+            minus_one_times(part(minus_dc2, hb, r), part(tc2, hb, r), part(go_so, hb, r))
 
         def cell_sum(r):
-            cols = cols_of(0)
-            nc.vector.tensor_tensor(out=c2_sb[:, r, :], in0=ip[:, r, cols], in1=fp[:, r, cols], op=ALU.add)
+            nc.vector.tensor_tensor(out=c2_sb[:, r, :], in0=part(ip, 0, r), in1=part(fp, 0, r), op=ALU.add)
+
+        def cell_sum_on_tensor(hb, r):
+            c2 = psum.tile([P, PACK, M_TILE], F32, name="acc")
+            nc.tensor.matmul(out=c2[:], lhsT=identity[:], rhs=part(ip, hb, r), start=True, stop=False)
+            nc.tensor.matmul(out=c2[:], lhsT=identity[:], rhs=part(fp, hb, r), start=False, stop=True)
+            return c2
 
         def cell_tanh(hb, r, c2):
-            cols = cols_of(hb)
-            nc.scalar.activation(out=minus_tc[:, r, cols], in_=c2, func=FUNC.Tanh, scale=-1.0)
-            nc.scalar.activation(out=minus_dc2[:, r, cols], in_=minus_tc[:, r, cols], func=FUNC.Square)
+            nc.scalar.activation(out=part(minus_tc, hb, r), in_=c2, func=FUNC.Tanh, scale=-1.0)
 
         last_product = {
             GATE_O: (minus_do_tc, minus_tc),
@@ -175,8 +208,8 @@ def tile_dependency_pa_v_kernel(
             r = slice(c * PACK, (c + 1) * PACK)
             nc.vector.tensor_tensor(
                 out=by_column_grouped(dg_grouped[:, hb, c, g, :, :]),
-                in0=by_column(in0[:, r, cols_of(hb)]),
-                in1=by_column(in1[:, r, cols_of(hb)]),
+                in0=by_column(part(in0, hb, r)),
+                in1=by_column(part(in1, hb, r)),
                 op=ALU.mult,
             )
 
@@ -213,31 +246,25 @@ def tile_dependency_pa_v_kernel(
                 multiply(acc, hb, g, n, c)
             return acc
 
-        rows = [slice(first, first + PIECE) for first in range(0, ROWS, PIECE)]
         by_pass = [slice(c * PACK, (c + 1) * PACK) for c in range(PASSES)]
         act = nc.scalar.copy
         vec = nc.vector.tensor_copy
-
-        def input_parts(hb, r):
-            product(ip, si, tg, hb, r)
-            minus_one_times(minus_g, minus_g, si, hb, r)
-            minus_one_times(minus_i, si, ip, hb, r)
-
-        def output_parts(hb, r):
-            product(go_so, so, go_sb, hb, r)
-            minus_one_times(minus_do_tc, so, go_so, hb, r)
 
         def load_gt(c, n):
             for s in streams_of(n):
                 load(stream_sb[s], streams[s], c)
 
-        load(gf_sb, gf, 0, 0, PIECE)
+        def rows(first, n):
+            return slice(first, first + n)
+
+        load(gf_sb, gf, 0, 0, 1)
         load(cell_sb, c0[0, :, :], 0)
-        load(gf_sb, gf, 0, PIECE, PIECE)
+        load(gf_sb, gf, 0, 1, 1)
+        load(gf_sb, gf, 0, 2, 2)
         load(go_sb, grad_out[:, 0:H], 0)
-        load(gf_sb, gf, 1, 0, PIECE)
+        load(gf_sb, gf, 1, 0, 2)
         load(cell_sb, c0[0, :, :], 1)
-        load(gf_sb, gf, 1, PIECE, PIECE)
+        load(gf_sb, gf, 1, 2, 2)
         load_gt(0, 0)
         load(go_sb, grad_out[:, 0:H], 1)
         load_gt(1, 0)
@@ -245,99 +272,111 @@ def tile_dependency_pa_v_kernel(
             for c in range(PASSES):
                 load_gt(c, n)
 
-        gate_activations(0, rows[0])
-        gate_activations(1, rows[0])
-        input_parts(0, rows[0])
-        product(fp, sf, cell_sb, 0, rows[0])
-        input_parts(1, rows[0])
-        minus_one_times(minus_f, sf, fp, 0, rows[0])
-        product(fp, sf, cell_sb, 1, rows[0])
-        cell_sum(rows[0])
-        minus_one_times(minus_f, sf, fp, 1, rows[0])
-        gate_activations(0, rows[1])
-        input_parts(0, rows[1])
-        product(fp, sf, cell_sb, 0, rows[1])
-        output_parts(0, rows[0])
-        cell_sum(rows[1])
-        minus_one_times(minus_f, sf, fp, 0, rows[1])
-        output_parts(0, rows[1])
-        gate_activations(1, rows[1])
+        for r in (rows(0, 1), rows(1, 1)):
+            gate_activations(None, r)
+            make_ip(None, r)
+            make_fp(None, r)
+            make_minus_i(None, r)
+            make_minus_f(None, r)
+            make_minus_g(None, r)
+        gate_activations(0, rows(2, 2))
+        make_ip(0, rows(2, 2))
+        make_fp(0, rows(2, 2))
+        make_go_so(0, by_pass[0])
+        cell_sum(by_pass[0])
+        make_minus_g(0, rows(2, 2))
+        make_minus_i(0, rows(2, 2))
+        make_minus_do_tc(0, by_pass[0])
+        make_minus_f(0, rows(2, 2))
+        gate_activations(1, rows(2, 2))
         cell_tanh(0, by_pass[0], c2_sb[:, by_pass[0], :])
+        activate(si, GATE_I, FUNC.Sigmoid, 0, rows(4, 2))
+        square(tc2, minus_tc, 0, by_pass[0])
         finish(0, GATE_O, 0)
-        minus_one_times(minus_dc2, minus_dc2, go_so, 0, by_pass[0])
-        gate_activations(0, rows[2])
-        product(ip, si, tg, 0, rows[2])
+        make_minus_dc2(0, by_pass[0])
+        activate(tg, GATE_G, FUNC.Tanh, 0, rows(4, 2))
+        activate(sf, GATE_F, FUNC.Sigmoid, 0, rows(4, 2))
+        make_ip(0, rows(4, 2))
         for g in FINISH_ORDER[1:]:
             finish(0, g, 0)
-        gate_activations(1, rows[2])
-        gate_activations(0, rows[3])
-        gate_activations(1, rows[3])
-        product(fp, sf, cell_sb, 0, rows[2])
+        square(tg2, tg, 0, rows(4, 2))
+        activate(so, GATE_O, FUNC.Sigmoid, 0, rows(4, 2))
+        gate_activations(0, rows(6, 2))
+        make_fp(0, rows(4, 2))
         quantise_dg(0, 0, slice(0, GATES))
-        product(ip, si, tg, 0, rows[3])
-        product(fp, sf, cell_sb, 0, rows[3])
+        make_ip(0, rows(6, 2))
+        make_fp(0, rows(6, 2))
+        make_minus_g(0, by_pass[1])
         cell_sum(by_pass[1])
-        g00 = new_gt_grouped()
-        regroup_gt(act, g00, 0, 0, 0, H)
+        g00 = regroup_tile(act, 0, 0)
         cell_tanh(0, by_pass[1], c2_sb[:, by_pass[1], :])
-        regroup_gt(act, g00, 0, 0, H, H)
-        minus_one_times(minus_i, si, ip, 0, by_pass[1])
-        minus_one_times(minus_f, sf, fp, 0, by_pass[1])
-        product(go_so, so, go_sb, 0, by_pass[1])
-        minus_one_times(minus_g, minus_g, si, 0, by_pass[1])
-        minus_one_times(minus_do_tc, so, go_so, 0, by_pass[1])
-        minus_one_times(minus_dc2, minus_dc2, go_so, 0, by_pass[1])
+        activate(si, GATE_I, FUNC.Sigmoid, 1, rows(4, 4))
+        square(tc2, minus_tc, 0, by_pass[1])
+        make_go_so(0, by_pass[1])
+        make_minus_i(0, by_pass[1])
+        make_minus_do_tc(0, by_pass[1])
+        make_minus_f(0, by_pass[1])
+        g10 = regroup_tile(act, 1, 0)
+        make_minus_dc2(0, by_pass[1])
         for g in FINISH_ORDER:
             finish(0, g, 1)
+        activate(tg, GATE_G, FUNC.Tanh, 1, rows(4, 4))
+        activate(sf, GATE_F, FUNC.Sigmoid, 1, rows(4, 4))
+        square(tg2, tg, 1, rows(4, 4))
+        activate(so, GATE_O, FUNC.Sigmoid, 1, rows(4, 4))
 
         quantise_gt(0, 0, g00)
-        rest = slice(PIECE, ROWS)
-        product(ip, si, tg, 1, rest)
-        quantise_dg(0, 1, slice(0, GATES))
-        g10 = regroup_tile(act, 1, 0)
-        product(fp, sf, cell_sb, 1, rest)
         quantise_gt(1, 0, g10)
+        quantise_dg(0, 1, slice(0, GATES))
         acc0 = [products_of(0, g, 0) for g in FINISH_ORDER]
-        c2_acc = []
-        for c in range(PASSES):
-            c2 = psum.tile([P, PACK, M_TILE], F32, name="acc")
-            k = by_pass[c]
-            nc.tensor.matmul(out=c2[:], lhsT=identity[:], rhs=ip[:, k, cols_of(1)], start=True, stop=False)
-            nc.tensor.matmul(out=c2[:], lhsT=identity[:], rhs=fp[:, k, cols_of(1)], start=False, stop=True)
-            c2_acc.append(c2)
         g01 = regroup_tile(act, 0, 1)
-        minus_one_times(minus_i, si, ip, 1, rest)
+        rest = rows(2, ROWS - 2)
+        make_ip(1, rest)
+        make_fp(1, rest)
+        c2_acc = [cell_sum_on_tensor(1, r) for r in by_pass]
         for g, acc in zip(FINISH_ORDER, acc0):
             store(act, acc, 0, g, 0)
-        minus_one_times(minus_f, sf, fp, 1, rest)
+        make_minus_i(1, rest)
+        make_minus_f(1, rest)
         quantise_gt(0, 1, g01)
         g02 = regroup_tile(vec, 0, 2)
-        product(go_so, so, go_sb, 1, slice(0, ROWS))
+        make_go_so(1, rows(0, ROWS))
         g11 = regroup_tile(act, 1, 1)
         for c in range(PASSES):
             cell_tanh(1, by_pass[c], c2_acc[c][:])
+        for c in range(PASSES):
+            square(tc2, minus_tc, 1, by_pass[c])
         quantise_gt(0, 2, g02)
+        make_minus_do_tc(1, rows(0, ROWS))
         quantise_gt(1, 1, g11)
         acc1 = [products_of(0, g, 1) for g in FINISH_ORDER]
         g12 = regroup_tile(vec, 1, 2)
         for g, acc in zip(FINISH_ORDER, acc1):
             store(act, acc, 0, g, 1)
-        minus_one_times(minus_do_tc, so, go_so, 1, slice(0, ROWS))
+        finish(1, GATE_O, 0)
         quantise_gt(1, 2, g12)
         acc2 = [products_of(0, g, 2) for g in FINISH_ORDER]
         for g, acc in zip(FINISH_ORDER, acc2):
             store(act, acc, 0, g, 2)
-        for g in FINISH_ORDER:
-            last = g == FINISH_ORDER[-1]
-            accs = [new_acc() for n in range(N_TILES)]
-            for c in range(PASSES):
-                finish(1, g, c)
-                if g == GATE_O and c == 0:
-                    minus_one_times(minus_dc2, minus_dc2, go_so, 1, slice(0, ROWS))
-                if g == GATE_F and c == 0:
-                    minus_one_times(minus_g, minus_g, si, 1, rest)
-                quantise_dg(1, c, slice(g, g + 1))
-                for n in range(N_TILES):
-                    multiply(accs[n], 1, g, n, c)
+        accs = {}
+        todo = [(g, c) for g in FINISH_ORDER for c in range(PASSES)]
+
+        def quantise_and_multiply(g, c):
+            quantise_dg(1, c, slice(g, g + 1))
+            if c == 0:
+                accs[g] = [new_acc() for n in range(N_TILES)]
             for n in range(N_TILES):
-                store(vec if last and n != 1 else act, accs[n], 1, g, n)
+                multiply(accs[g][n], 1, g, n, c)
+            if c == PASSES - 1:
+                for n in range(N_TILES):
+                    store(vec if g == FINISH_ORDER[-1] and n != 1 else act, accs[g][n], 1, g, n)
+
+        for k, (g, c) in enumerate(todo):
+            if k > 0:
+                if (g, c) == (GATE_G, 0):
+                    make_minus_g(1, rest)
+                if (g, c) == (GATE_O, 1):
+                    make_minus_dc2(1, rows(0, ROWS))
+                finish(1, g, c)
+                quantise_and_multiply(*todo[k - 1])
+        quantise_and_multiply(*todo[-1])

@@ -69,12 +69,14 @@ def tile_dependency_pa_v_kernel(
     with (
         tc.tile_pool(name="resident", bufs=1) as resident,
         tc.tile_pool(name="gt_grouped", bufs=4) as gt_grouped_pool,
-        tc.tile_pool(name="stage", bufs=8) as stage,
+        tc.tile_pool(name="stage", bufs=12) as stage,
         tc.psum_pool(name="psum", bufs=8) as psum,
         tc.manual_schedule(),
     ):
         identity = resident.tile([P, P], F32, name="identity")
         make_identity(nc, identity[:])
+        identity_bf16 = resident.tile([P, P], BF16, name="identity_bf16")
+        make_identity(nc, identity_bf16[:])
 
         gf_sb = resident.tile([P, ROWS, GATES * H], F32, name="gf_sb")
         cell_sb = resident.tile([P, ROWS, H], BF16, name="cell_sb")
@@ -116,6 +118,27 @@ def tile_dependency_pa_v_kernel(
                 regroup_gt(copy, gt_grouped, c, s, 0, widths[s])
             return gt_grouped
 
+        def regroup_on_tensor(c, s):
+            banks = []
+            for first in range(0, N_TILE, N_TILE // 2):
+                bank = psum.tile([P, N_TILE // 2, PACK], BF16, name="acc")
+                for t in range(0, PACK, 2):
+                    nc.tensor.matmul(
+                        out=bank[:, :, t : t + 2].rearrange("p w t -> p t w"),
+                        lhsT=identity_bf16[:],
+                        rhs=stream_sb[s][:, c * PACK + t : c * PACK + t + 2, first : first + N_TILE // 2],
+                        start=True,
+                        stop=True,
+                    )
+                banks.append(bank)
+            return banks
+
+        def regrouped(banks):
+            gt_grouped = new_gt_grouped()
+            for k, bank in enumerate(banks):
+                nc.scalar.copy(out=gt_grouped[:, k * (N_TILE // 2) : (k + 1) * (N_TILE // 2), :], in_=bank[:])
+            return gt_grouped
+
         def quantise_gt(c, n, gt_grouped):
             nc.vector.quantize_mx(
                 out=gt_codes[:, c, n, :].bitcast(E4M3_X4),
@@ -123,12 +146,11 @@ def tile_dependency_pa_v_kernel(
                 in_=gt_grouped[:].rearrange("p w t -> p (w t)"),
             )
 
-        names = ("si", "tg", "sf", "so", "tg2", "ip", "fp", "go_so", "minus_tc", "tc2")
-        si, tg, sf, so, tg2, ip, fp, go_so, minus_tc, tc2 = [
+        names = ("si", "tg", "sf", "so", "tg2", "ip", "fp", "minus_i", "go_so", "minus_tc", "tc2")
+        si, tg, sf, so, tg2, ip, fp, minus_i, go_so, minus_tc, tc2 = [
             resident.tile([P, H_BLOCKS, ROWS, M_TILE], F32, name=name) for name in names
         ]
-        minus_i, minus_f, minus_g, minus_do_tc, minus_dc2 = tg, sf, tg2, so, tc2
-        c2_sb = resident.tile([P, ROWS, M_TILE], F32, name="c2_sb")
+        minus_f, minus_g, minus_do_tc, minus_dc2 = sf, tg2, so, tc2
         dg_grouped = resident.tile(
             [P, H_BLOCKS, PASSES, GATES, M_TILE, PACK], BF16, name="dg_grouped", align_bytes=64
         )
@@ -184,8 +206,9 @@ def tile_dependency_pa_v_kernel(
         def make_minus_dc2(hb, r):
             minus_one_times(part(minus_dc2, hb, r), part(tc2, hb, r), part(go_so, hb, r))
 
-        def cell_sum(r):
-            nc.vector.tensor_tensor(out=c2_sb[:, r, :], in0=part(ip, 0, r), in1=part(fp, 0, r), op=ALU.add)
+        def cell_sum(hb, r):
+            nc.vector.tensor_tensor(out=part(minus_tc, hb, r), in0=part(ip, hb, r), in1=part(fp, hb, r), op=ALU.add)
+            return part(minus_tc, hb, r)
 
         def cell_sum_on_tensor(hb, r):
             c2 = psum.tile([P, PACK, M_TILE], F32, name="acc")
@@ -257,126 +280,151 @@ def tile_dependency_pa_v_kernel(
         def rows(first, n):
             return slice(first, first + n)
 
-        load(gf_sb, gf, 0, 0, 1)
+        def load_gf(first, n):
+            load(gf_sb, gf, first // PACK, first % PACK, n)
+
+        def cell_activations(hb, r):
+            activate(si, GATE_I, FUNC.Sigmoid, hb, r)
+            activate(tg, GATE_G, FUNC.Tanh, hb, r)
+            activate(sf, GATE_F, FUNC.Sigmoid, hb, r)
+
+        def output_activations(hb, r):
+            activate(so, GATE_O, FUNC.Sigmoid, hb, r)
+            square(tg2, tg, hb, r)
+
+        load_gf(0, 1)
         load(cell_sb, c0[0, :, :], 0)
-        load(gf_sb, gf, 0, 1, 1)
-        load(gf_sb, gf, 0, 2, 2)
+        load_gf(1, 1)
+        load_gf(2, 1)
+        load_gf(3, 1)
         load(go_sb, grad_out[:, 0:H], 0)
-        load(gf_sb, gf, 1, 0, 2)
+        load_gf(4, 2)
         load(cell_sb, c0[0, :, :], 1)
-        load(gf_sb, gf, 1, 2, 2)
+        load_gf(6, 2)
         load_gt(0, 0)
         load(go_sb, grad_out[:, 0:H], 1)
         load_gt(1, 0)
-        for n in (1, 2):
+        for n in (2, 1):
             for c in range(PASSES):
                 load_gt(c, n)
 
-        for r in (rows(0, 1), rows(1, 1)):
-            gate_activations(None, r)
+        for first in range(PACK):
+            r = rows(first, 1)
+            cell_activations(None, r)
             make_ip(None, r)
             make_fp(None, r)
             make_minus_i(None, r)
+            if first == PACK - 1:
+                c2_00 = cell_sum(0, by_pass[0])
+                output_activations(None, by_pass[0])
             make_minus_f(None, r)
-            make_minus_g(None, r)
-        gate_activations(0, rows(2, 2))
-        make_ip(0, rows(2, 2))
-        make_fp(0, rows(2, 2))
         make_go_so(0, by_pass[0])
-        cell_sum(by_pass[0])
-        make_minus_g(0, rows(2, 2))
-        make_minus_i(0, rows(2, 2))
+        make_minus_g(0, by_pass[0])
         make_minus_do_tc(0, by_pass[0])
-        make_minus_f(0, rows(2, 2))
-        gate_activations(1, rows(2, 2))
-        cell_tanh(0, by_pass[0], c2_sb[:, by_pass[0], :])
+        cell_tanh(0, by_pass[0], c2_00)
         activate(si, GATE_I, FUNC.Sigmoid, 0, rows(4, 2))
         square(tc2, minus_tc, 0, by_pass[0])
         finish(0, GATE_O, 0)
         make_minus_dc2(0, by_pass[0])
         activate(tg, GATE_G, FUNC.Tanh, 0, rows(4, 2))
         activate(sf, GATE_F, FUNC.Sigmoid, 0, rows(4, 2))
+        c2_10 = cell_sum_on_tensor(1, by_pass[0])
         make_ip(0, rows(4, 2))
         for g in FINISH_ORDER[1:]:
             finish(0, g, 0)
-        square(tg2, tg, 0, rows(4, 2))
-        activate(so, GATE_O, FUNC.Sigmoid, 0, rows(4, 2))
-        gate_activations(0, rows(6, 2))
+        output_activations(0, rows(4, 2))
+        cell_activations(0, rows(6, 2))
+        output_activations(0, rows(6, 2))
         make_fp(0, rows(4, 2))
         quantise_dg(0, 0, slice(0, GATES))
         make_ip(0, rows(6, 2))
         make_fp(0, rows(6, 2))
         make_minus_g(0, by_pass[1])
-        cell_sum(by_pass[1])
-        g00 = regroup_tile(act, 0, 0)
-        cell_tanh(0, by_pass[1], c2_sb[:, by_pass[1], :])
-        activate(si, GATE_I, FUNC.Sigmoid, 1, rows(4, 4))
+        c2_01 = cell_sum(0, by_pass[1])
+        cell_activations(1, by_pass[1])
+        cell_tanh(0, by_pass[1], c2_01)
+        output_activations(1, by_pass[1])
         square(tc2, minus_tc, 0, by_pass[1])
+        cell_tanh(1, by_pass[0], c2_10[:])
+        g00 = regrouped(regroup_on_tensor(0, 0))
+        square(tc2, minus_tc, 1, by_pass[0])
         make_go_so(0, by_pass[1])
         make_minus_i(0, by_pass[1])
         make_minus_do_tc(0, by_pass[1])
         make_minus_f(0, by_pass[1])
-        g10 = regroup_tile(act, 1, 0)
+        make_minus_g(1, by_pass[0])
         make_minus_dc2(0, by_pass[1])
+        g10 = regrouped(regroup_on_tensor(1, 0))
         for g in FINISH_ORDER:
             finish(0, g, 1)
-        activate(tg, GATE_G, FUNC.Tanh, 1, rows(4, 4))
-        activate(sf, GATE_F, FUNC.Sigmoid, 1, rows(4, 4))
-        square(tg2, tg, 1, rows(4, 4))
-        activate(so, GATE_O, FUNC.Sigmoid, 1, rows(4, 4))
 
+        g12 = regroup_tile(act, 1, 2)
         quantise_gt(0, 0, g00)
         quantise_gt(1, 0, g10)
         quantise_dg(0, 1, slice(0, GATES))
+        g01 = regrouped(regroup_on_tensor(0, 1))
         acc0 = [products_of(0, g, 0) for g in FINISH_ORDER]
-        g01 = regroup_tile(act, 0, 1)
-        rest = rows(2, ROWS - 2)
-        make_ip(1, rest)
-        make_fp(1, rest)
-        c2_acc = [cell_sum_on_tensor(1, r) for r in by_pass]
+        make_ip(1, by_pass[1])
+        make_fp(1, by_pass[1])
+        g02 = regroup_tile(vec, 0, 2)
+        c2_11 = cell_sum_on_tensor(1, by_pass[1])
         for g, acc in zip(FINISH_ORDER, acc0):
             store(act, acc, 0, g, 0)
-        make_minus_i(1, rest)
-        make_minus_f(1, rest)
-        quantise_gt(0, 1, g01)
-        g02 = regroup_tile(vec, 0, 2)
-        make_go_so(1, rows(0, ROWS))
         g11 = regroup_tile(act, 1, 1)
-        for c in range(PASSES):
-            cell_tanh(1, by_pass[c], c2_acc[c][:])
-        for c in range(PASSES):
-            square(tc2, minus_tc, 1, by_pass[c])
+        quantise_gt(1, 2, g12)
         quantise_gt(0, 2, g02)
+        make_go_so(1, rows(0, ROWS))
+        acc2 = [products_of(0, g, 2) for g in FINISH_ORDER]
+        cell_tanh(1, by_pass[1], c2_11[:])
+        for g, acc in list(zip(FINISH_ORDER, acc2))[:1]:
+            store(act, acc, 0, g, 2)
+        square(tc2, minus_tc, 1, by_pass[1])
+        for g, acc in list(zip(FINISH_ORDER, acc2))[1:]:
+            store(act, acc, 0, g, 2)
+        quantise_gt(0, 1, g01)
         make_minus_do_tc(1, rows(0, ROWS))
+        make_minus_i(1, by_pass[1])
         quantise_gt(1, 1, g11)
         acc1 = [products_of(0, g, 1) for g in FINISH_ORDER]
-        g12 = regroup_tile(vec, 1, 2)
         for g, acc in zip(FINISH_ORDER, acc1):
             store(act, acc, 0, g, 1)
-        finish(1, GATE_O, 0)
-        quantise_gt(1, 2, g12)
-        acc2 = [products_of(0, g, 2) for g in FINISH_ORDER]
-        for g, acc in zip(FINISH_ORDER, acc2):
-            store(act, acc, 0, g, 2)
+
         accs = {}
-        todo = [(g, c) for g in FINISH_ORDER for c in range(PASSES)]
 
         def quantise_and_multiply(g, c):
             quantise_dg(1, c, slice(g, g + 1))
+            multiply_last(g, c)
+
+        def multiply_last(g, c):
             if c == 0:
                 accs[g] = [new_acc() for n in range(N_TILES)]
             for n in range(N_TILES):
                 multiply(accs[g][n], 1, g, n, c)
-            if c == PASSES - 1:
-                for n in range(N_TILES):
-                    store(vec if g == FINISH_ORDER[-1] and n != 1 else act, accs[g][n], 1, g, n)
 
-        for k, (g, c) in enumerate(todo):
-            if k > 0:
-                if (g, c) == (GATE_G, 0):
-                    make_minus_g(1, rest)
-                if (g, c) == (GATE_O, 1):
-                    make_minus_dc2(1, rows(0, ROWS))
-                finish(1, g, c)
-                quantise_and_multiply(*todo[k - 1])
-        quantise_and_multiply(*todo[-1])
+        def store_last(g):
+            for n in range(N_TILES):
+                store(vec if g == FINISH_ORDER[-1] and n != 1 else act, accs[g][n], 1, g, n)
+
+        finish(1, GATE_O, 0)
+        finish(1, GATE_O, 1)
+        quantise_and_multiply(GATE_O, 0)
+        make_minus_dc2(1, rows(0, ROWS))
+        quantise_and_multiply(GATE_O, 1)
+        store_last(GATE_O)
+        finish(1, GATE_I, 0)
+        finish(1, GATE_I, 1)
+        quantise_and_multiply(GATE_I, 0)
+        make_minus_f(1, by_pass[1])
+        quantise_and_multiply(GATE_I, 1)
+        store_last(GATE_I)
+        finish(1, GATE_F, 0)
+        finish(1, GATE_F, 1)
+        quantise_and_multiply(GATE_F, 0)
+        make_minus_g(1, by_pass[1])
+        quantise_and_multiply(GATE_F, 1)
+        store_last(GATE_F)
+        finish(1, GATE_G, 0)
+        quantise_and_multiply(GATE_G, 0)
+        finish(1, GATE_G, 1)
+        quantise_and_multiply(GATE_G, 1)
+        store_last(GATE_G)

@@ -68,8 +68,9 @@ def tile_dependency_pa_v_kernel(
     nc = tc.nc
     with (
         tc.tile_pool(name="resident", bufs=1) as resident,
+        tc.tile_pool(name="dg_grouped", bufs=2) as dg_grouped_pool,
         tc.tile_pool(name="gt_grouped", bufs=4) as gt_grouped_pool,
-        tc.tile_pool(name="stage", bufs=12) as stage,
+        tc.tile_pool(name="stage", bufs=14) as stage,
         tc.psum_pool(name="psum", bufs=8) as psum,
         tc.manual_schedule(),
     ):
@@ -151,9 +152,10 @@ def tile_dependency_pa_v_kernel(
             resident.tile([P, H_BLOCKS, ROWS, M_TILE], F32, name=name) for name in names
         ]
         minus_f, minus_g, minus_do_tc, minus_dc2 = sf, tg2, so, tc2
-        dg_grouped = resident.tile(
-            [P, H_BLOCKS, PASSES, GATES, M_TILE, PACK], BF16, name="dg_grouped", align_bytes=64
-        )
+        dg_grouped = [
+            dg_grouped_pool.tile([P, PASSES, GATES, M_TILE, PACK], BF16, name="dg_grouped", align_bytes=64)
+            for hb in range(H_BLOCKS)
+        ]
 
         def part(t, hb, r):
             return t[:, :, r, :] if hb is None else t[:, hb, r, :]
@@ -230,7 +232,7 @@ def tile_dependency_pa_v_kernel(
             in0, in1 = last_product[g]
             r = slice(c * PACK, (c + 1) * PACK)
             nc.vector.tensor_tensor(
-                out=by_column_grouped(dg_grouped[:, hb, c, g, :, :]),
+                out=by_column_grouped(dg_grouped[hb][:, c, g, :, :]),
                 in0=by_column(part(in0, hb, r)),
                 in1=by_column(part(in1, hb, r)),
                 op=ALU.mult,
@@ -240,7 +242,7 @@ def tile_dependency_pa_v_kernel(
             nc.vector.quantize_mx(
                 out=dg_codes[:, hb, c, gates, :].rearrange("p g m -> p (g m)").bitcast(E5M2_X4),
                 scales=dg_scales[:, hb, c, gates, :].rearrange("p g m -> p (g m)"),
-                in_=dg_grouped[:, hb, c, gates, :, :].rearrange("p g m t -> p (g m t)"),
+                in_=dg_grouped[hb][:, c, gates, :, :].rearrange("p g m t -> p (g m t)"),
             )
 
         def new_acc():
@@ -295,8 +297,7 @@ def tile_dependency_pa_v_kernel(
         load_gf(0, 1)
         load(cell_sb, c0[0, :, :], 0)
         load_gf(1, 1)
-        load_gf(2, 1)
-        load_gf(3, 1)
+        load_gf(2, 2)
         load(go_sb, grad_out[:, 0:H], 0)
         load_gf(4, 2)
         load(cell_sb, c0[0, :, :], 1)
@@ -304,35 +305,43 @@ def tile_dependency_pa_v_kernel(
         load_gt(0, 0)
         load(go_sb, grad_out[:, 0:H], 1)
         load_gt(1, 0)
-        for n in (2, 1):
+        for n in (1, 2):
             for c in range(PASSES):
                 load_gt(c, n)
 
-        for first in range(PACK):
+        for first in range(2):
             r = rows(first, 1)
             cell_activations(None, r)
             make_ip(None, r)
             make_fp(None, r)
             make_minus_i(None, r)
-            if first == PACK - 1:
-                c2_00 = cell_sum(0, by_pass[0])
-                output_activations(None, by_pass[0])
             make_minus_f(None, r)
-        make_go_so(0, by_pass[0])
-        make_minus_g(0, by_pass[0])
+        output_activations(None, rows(0, 2))
+        make_minus_g(None, rows(0, 2))
+        cell_activations(0, rows(2, 2))
+        output_activations(0, rows(2, 2))
+        make_ip(0, rows(2, 2))
+        make_fp(0, rows(2, 2))
+        make_go_so(0, rows(0, 2))
+        c2_00 = cell_sum(0, by_pass[0])
+        make_minus_i(0, rows(2, 2))
+        make_minus_f(0, rows(2, 2))
+        make_go_so(0, rows(2, 2))
+        make_minus_g(0, rows(2, 2))
         make_minus_do_tc(0, by_pass[0])
+        cell_activations(1, rows(2, 2))
         cell_tanh(0, by_pass[0], c2_00)
         activate(si, GATE_I, FUNC.Sigmoid, 0, rows(4, 2))
         square(tc2, minus_tc, 0, by_pass[0])
+        make_go_so(1, rows(0, 2))
         finish(0, GATE_O, 0)
         make_minus_dc2(0, by_pass[0])
         activate(tg, GATE_G, FUNC.Tanh, 0, rows(4, 2))
         activate(sf, GATE_F, FUNC.Sigmoid, 0, rows(4, 2))
-        c2_10 = cell_sum_on_tensor(1, by_pass[0])
+        output_activations(0, rows(4, 2))
         make_ip(0, rows(4, 2))
         for g in FINISH_ORDER[1:]:
             finish(0, g, 0)
-        output_activations(0, rows(4, 2))
         cell_activations(0, rows(6, 2))
         output_activations(0, rows(6, 2))
         make_fp(0, rows(4, 2))
@@ -341,59 +350,64 @@ def tile_dependency_pa_v_kernel(
         make_fp(0, rows(6, 2))
         make_minus_g(0, by_pass[1])
         c2_01 = cell_sum(0, by_pass[1])
+        output_activations(1, rows(2, 2))
         cell_activations(1, by_pass[1])
+        activate(so, GATE_O, FUNC.Sigmoid, 1, by_pass[1])
         cell_tanh(0, by_pass[1], c2_01)
-        output_activations(1, by_pass[1])
+        square(tg2, tg, 1, by_pass[1])
         square(tc2, minus_tc, 0, by_pass[1])
-        cell_tanh(1, by_pass[0], c2_10[:])
         g00 = regrouped(regroup_on_tensor(0, 0))
-        square(tc2, minus_tc, 1, by_pass[0])
         make_go_so(0, by_pass[1])
         make_minus_i(0, by_pass[1])
         make_minus_do_tc(0, by_pass[1])
         make_minus_f(0, by_pass[1])
-        make_minus_g(1, by_pass[0])
+        make_ip(1, rows(2, 2))
+        finish(0, GATE_O, 1)
+        make_fp(1, rows(2, 2))
         make_minus_dc2(0, by_pass[1])
-        g10 = regrouped(regroup_on_tensor(1, 0))
-        for g in FINISH_ORDER:
-            finish(0, g, 1)
-
-        g12 = regroup_tile(act, 1, 2)
         quantise_gt(0, 0, g00)
+        g10 = regrouped(regroup_on_tensor(1, 0))
+        for g in FINISH_ORDER[1:]:
+            finish(0, g, 1)
         quantise_gt(1, 0, g10)
         quantise_dg(0, 1, slice(0, GATES))
+
         g01 = regrouped(regroup_on_tensor(0, 1))
+        c2_10 = cell_sum_on_tensor(1, by_pass[0])
+        g11 = regroup_tile(act, 1, 1)
         acc0 = [products_of(0, g, 0) for g in FINISH_ORDER]
         make_ip(1, by_pass[1])
         make_fp(1, by_pass[1])
-        g02 = regroup_tile(vec, 0, 2)
-        c2_11 = cell_sum_on_tensor(1, by_pass[1])
+        make_minus_i(1, rows(2, 2))
+        make_minus_f(1, rows(2, 2))
+        make_minus_g(1, rows(2, 2))
         for g, acc in zip(FINISH_ORDER, acc0):
             store(act, acc, 0, g, 0)
-        g11 = regroup_tile(act, 1, 1)
-        quantise_gt(1, 2, g12)
-        quantise_gt(0, 2, g02)
-        make_go_so(1, rows(0, ROWS))
-        acc2 = [products_of(0, g, 2) for g in FINISH_ORDER]
-        cell_tanh(1, by_pass[1], c2_11[:])
-        for g, acc in list(zip(FINISH_ORDER, acc2))[:1]:
-            store(act, acc, 0, g, 2)
-        square(tc2, minus_tc, 1, by_pass[1])
-        for g, acc in list(zip(FINISH_ORDER, acc2))[1:]:
-            store(act, acc, 0, g, 2)
         quantise_gt(0, 1, g01)
-        make_minus_do_tc(1, rows(0, ROWS))
-        make_minus_i(1, by_pass[1])
         quantise_gt(1, 1, g11)
         acc1 = [products_of(0, g, 1) for g in FINISH_ORDER]
-        for g, acc in zip(FINISH_ORDER, acc1):
+        c2_11 = cell_sum_on_tensor(1, by_pass[1])
+        g02 = regroup_tile(vec, 0, 2)
+        g12 = regroup_tile(act, 1, 2)
+        quantise_gt(0, 2, g02)
+        cell_tanh(1, by_pass[0], c2_10[:])
+        for k, (g, acc) in enumerate(zip(FINISH_ORDER, acc1)):
             store(act, acc, 0, g, 1)
+            if k == 0:
+                square(tc2, minus_tc, 1, by_pass[0])
+            if k == 2:
+                cell_tanh(1, by_pass[1], c2_11[:])
+        square(tc2, minus_tc, 1, by_pass[1])
+        make_go_so(1, rows(2, 2))
+        make_minus_i(1, by_pass[1])
+        make_go_so(1, by_pass[1])
+        make_minus_do_tc(1, by_pass[0])
+        quantise_gt(1, 2, g12)
+        make_minus_do_tc(1, by_pass[1])
+        for g in FINISH_ORDER:
+            store(act, products_of(0, g, 2), 0, g, 2)
 
         accs = {}
-
-        def quantise_and_multiply(g, c):
-            quantise_dg(1, c, slice(g, g + 1))
-            multiply_last(g, c)
 
         def multiply_last(g, c):
             if c == 0:
@@ -401,14 +415,19 @@ def tile_dependency_pa_v_kernel(
             for n in range(N_TILES):
                 multiply(accs[g][n], 1, g, n, c)
 
+        def quantise_and_multiply(g, c):
+            quantise_dg(1, c, slice(g, g + 1))
+            multiply_last(g, c)
+
         def store_last(g):
             for n in range(N_TILES):
                 store(vec if g == FINISH_ORDER[-1] and n != 1 else act, accs[g][n], 1, g, n)
 
         finish(1, GATE_O, 0)
+        make_minus_dc2(1, by_pass[0])
         finish(1, GATE_O, 1)
         quantise_and_multiply(GATE_O, 0)
-        make_minus_dc2(1, rows(0, ROWS))
+        make_minus_dc2(1, by_pass[1])
         quantise_and_multiply(GATE_O, 1)
         store_last(GATE_O)
         finish(1, GATE_I, 0)

@@ -134,10 +134,13 @@ def tile_dependency_pa_v_kernel(
                 banks.append(bank)
             return banks
 
+        def copy_bank(gt_grouped, banks, k):
+            nc.scalar.copy(out=gt_grouped[:, k * (N_TILE // 2) : (k + 1) * (N_TILE // 2), :], in_=banks[k][:])
+
         def regrouped(banks):
             gt_grouped = new_gt_grouped()
-            for k, bank in enumerate(banks):
-                nc.scalar.copy(out=gt_grouped[:, k * (N_TILE // 2) : (k + 1) * (N_TILE // 2), :], in_=bank[:])
+            for k in range(len(banks)):
+                copy_bank(gt_grouped, banks, k)
             return gt_grouped
 
         def quantise_gt(c, n, gt_grouped):
@@ -295,9 +298,10 @@ def tile_dependency_pa_v_kernel(
             square(tg2, tg, hb, r)
 
         load_gf(0, 1)
-        load(cell_sb, c0[0, :, :], 0)
+        load(cell_sb, c0[0, :, :], 0, 0, 2)
         load_gf(1, 1)
         load_gf(2, 2)
+        load(cell_sb, c0[0, :, :], 0, 2, 2)
         load(go_sb, grad_out[:, 0:H], 0)
         load_gf(4, 2)
         load(cell_sb, c0[0, :, :], 1)
@@ -389,6 +393,7 @@ def tile_dependency_pa_v_kernel(
         c2_11 = cell_sum_on_tensor(1, by_pass[1])
         g02 = regroup_tile(vec, 0, 2)
         g12 = regroup_tile(act, 1, 2)
+        make_go_so(1, rows(2, 2))
         quantise_gt(0, 2, g02)
         cell_tanh(1, by_pass[0], c2_10[:])
         for k, (g, acc) in enumerate(zip(FINISH_ORDER, acc1)):
@@ -398,7 +403,6 @@ def tile_dependency_pa_v_kernel(
             if k == 2:
                 cell_tanh(1, by_pass[1], c2_11[:])
         square(tc2, minus_tc, 1, by_pass[1])
-        make_go_so(1, rows(2, 2))
         make_minus_i(1, by_pass[1])
         make_go_so(1, by_pass[1])
         make_minus_do_tc(1, by_pass[0])
@@ -425,24 +429,24 @@ def tile_dependency_pa_v_kernel(
 
         finish(1, GATE_O, 0)
         make_minus_dc2(1, by_pass[0])
-        finish(1, GATE_O, 1)
         quantise_and_multiply(GATE_O, 0)
+        make_minus_f(1, by_pass[1])
+        finish(1, GATE_O, 1)
         make_minus_dc2(1, by_pass[1])
         quantise_and_multiply(GATE_O, 1)
         store_last(GATE_O)
         finish(1, GATE_I, 0)
         finish(1, GATE_I, 1)
         quantise_and_multiply(GATE_I, 0)
-        make_minus_f(1, by_pass[1])
         quantise_and_multiply(GATE_I, 1)
         store_last(GATE_I)
         finish(1, GATE_F, 0)
         finish(1, GATE_F, 1)
         quantise_and_multiply(GATE_F, 0)
-        make_minus_g(1, by_pass[1])
+        finish(1, GATE_G, 0)
         quantise_and_multiply(GATE_F, 1)
         store_last(GATE_F)
-        finish(1, GATE_G, 0)
+        make_minus_g(1, by_pass[1])
         quantise_and_multiply(GATE_G, 0)
         finish(1, GATE_G, 1)
         quantise_and_multiply(GATE_G, 1)

@@ -326,11 +326,10 @@ def tile_dependency_pa_v_kernel(
         output_activations(0, rows(2, 2))
         make_ip(0, rows(2, 2))
         make_fp(0, rows(2, 2))
-        make_go_so(0, rows(0, 2))
-        c2_00 = cell_sum(0, by_pass[0])
         make_minus_i(0, rows(2, 2))
+        c2_00 = cell_sum(0, by_pass[0])
         make_minus_f(0, rows(2, 2))
-        make_go_so(0, rows(2, 2))
+        make_go_so(0, by_pass[0])
         make_minus_g(0, rows(2, 2))
         make_minus_do_tc(0, by_pass[0])
         cell_activations(1, rows(2, 2))
@@ -346,6 +345,7 @@ def tile_dependency_pa_v_kernel(
         make_ip(0, rows(4, 2))
         for g in FINISH_ORDER[1:]:
             finish(0, g, 0)
+        output_activations(1, rows(2, 2))
         cell_activations(0, rows(6, 2))
         output_activations(0, rows(6, 2))
         make_fp(0, rows(4, 2))
@@ -354,13 +354,14 @@ def tile_dependency_pa_v_kernel(
         make_fp(0, rows(6, 2))
         make_minus_g(0, by_pass[1])
         c2_01 = cell_sum(0, by_pass[1])
-        output_activations(1, rows(2, 2))
+        b00 = regroup_on_tensor(0, 0)
+        g00 = new_gt_grouped()
         cell_activations(1, by_pass[1])
-        activate(so, GATE_O, FUNC.Sigmoid, 1, by_pass[1])
+        output_activations(1, by_pass[1])
         cell_tanh(0, by_pass[1], c2_01)
-        square(tg2, tg, 1, by_pass[1])
+        copy_bank(g00, b00, 0)
         square(tc2, minus_tc, 0, by_pass[1])
-        g00 = regrouped(regroup_on_tensor(0, 0))
+        copy_bank(g00, b00, 1)
         make_go_so(0, by_pass[1])
         make_minus_i(0, by_pass[1])
         make_minus_do_tc(0, by_pass[1])

@@ -383,8 +383,6 @@ def tile_dependency_pa_v_kernel(
         acc0 = [products_of(0, g, 0) for g in FINISH_ORDER]
         make_ip(1, by_pass[1])
         make_fp(1, by_pass[1])
-        make_minus_i(1, rows(2, 2))
-        make_minus_f(1, rows(2, 2))
         make_minus_g(1, rows(2, 2))
         for g, acc in zip(FINISH_ORDER, acc0):
             store(act, acc, 0, g, 0)
@@ -394,7 +392,7 @@ def tile_dependency_pa_v_kernel(
         c2_11 = cell_sum_on_tensor(1, by_pass[1])
         g02 = regroup_tile(vec, 0, 2)
         g12 = regroup_tile(act, 1, 2)
-        make_go_so(1, rows(2, 2))
+        make_minus_i(1, rows(2, ROWS - 2))
         quantise_gt(0, 2, g02)
         cell_tanh(1, by_pass[0], c2_10[:])
         for k, (g, acc) in enumerate(zip(FINISH_ORDER, acc1)):
@@ -404,10 +402,9 @@ def tile_dependency_pa_v_kernel(
             if k == 2:
                 cell_tanh(1, by_pass[1], c2_11[:])
         square(tc2, minus_tc, 1, by_pass[1])
-        make_minus_i(1, by_pass[1])
-        make_go_so(1, by_pass[1])
-        make_minus_do_tc(1, by_pass[0])
+        make_go_so(1, rows(2, ROWS - 2))
         quantise_gt(1, 2, g12)
+        make_minus_do_tc(1, by_pass[0])
         make_minus_do_tc(1, by_pass[1])
         for g in FINISH_ORDER:
             store(act, products_of(0, g, 2), 0, g, 2)
@@ -431,7 +428,7 @@ def tile_dependency_pa_v_kernel(
         finish(1, GATE_O, 0)
         make_minus_dc2(1, by_pass[0])
         quantise_and_multiply(GATE_O, 0)
-        make_minus_f(1, by_pass[1])
+        make_minus_f(1, rows(2, ROWS - 2))
         finish(1, GATE_O, 1)
         make_minus_dc2(1, by_pass[1])
         quantise_and_multiply(GATE_O, 1)

import concourse.mybir as mybir
from concourse.masks import make_identity

F32 = mybir.dt.float32
BF16 = mybir.dt.bfloat16
U32 = mybir.dt.uint32
U8 = mybir.dt.uint8
E4M3_X4 = mybir.dt.float8_e4m3fn_x4
E5M2_X4 = mybir.dt.float8_e5m2_x4
FUNC = mybir.ActivationFunctionType
ALU = mybir.AluOpType

P = 128
PACK = 4
K_PASS = P * PACK
TOKENS = 1024
PASSES = TOKENS // K_PASS
ROWS = PASSES * PACK
PIECE = 2
H = 256
GATE_I, GATE_F, GATE_G, GATE_O = 0, 1, 2, 3
GATES = 4
FINISH_ORDER = (GATE_O, GATE_I, GATE_F, GATE_G)
M_TILE = 128
H_BLOCKS = H // M_TILE
N_TILE = 512
N_TILES = 3
RUN = 4

FLOPS = 2 * TOKENS * (GATES * H) * (N_TILES * N_TILE)
BYTES = (
    TOKENS * N_TILES * N_TILE * 2
    + TOKENS * GATES * H * 4
    + 2 * TOKENS * H * 2
    + GATES * H * N_TILES * N_TILE * 4
)


def by_column(rows_first):
    return rows_first.rearrange("p t (q i) -> p q t i", i=RUN)


def by_column_grouped(columns_first):
    return columns_first.rearrange("p (q i) t -> p q t i", i=RUN)


def tile_dependency_pa_v_kernel(
    tc,
    hn_chunks,
    hn_tags,
    x,
    tags,
    chunks,
    h0,
    c0,
    wih_f,
    whh_f,
    bih_f,
    bhh_f,
    wih_b,
    whh_b,
    bih_b,
    bhh_b,
    gf,
    grad_out,
    out,
):
    nc = tc.nc
    with (
        tc.tile_pool(name="resident", bufs=1) as resident,
        tc.tile_pool(name="dg_grouped", bufs=2) as dg_grouped_pool,
        tc.tile_pool(name="gt_grouped", bufs=4) as gt_grouped_pool,
        tc.tile_pool(name="stage", bufs=14) as stage,
        tc.psum_pool(name="psum", bufs=8) as psum,
        tc.manual_schedule(),
    ):
        identity = resident.tile([P, P], F32, name="identity")
        make_identity(nc, identity[:])
        identity_bf16 = resident.tile([P, P], BF16, name="identity_bf16")
        make_identity(nc, identity_bf16[:])

        gf_sb = resident.tile([P, ROWS, GATES * H], F32, name="gf_sb")
        cell_sb = resident.tile([P, ROWS, H], BF16, name="cell_sb")
        go_sb = resident.tile([P, ROWS, H], BF16, name="go_sb")
        streams = (hn_chunks, hn_tags, x, tags, chunks)
        widths = [stream.shape[1] for stream in streams]
        first_cols = [sum(widths[:s]) for s in range(len(streams))]
        stream_sb = [resident.tile([P, ROWS, widths[s]], BF16, name="stream_sb%d" % s) for s in range(len(streams))]

        def streams_of(n):
            return [s for s in range(len(streams)) if first_cols[s] // N_TILE == n]

        def load(dst, src, c, first=0, n_rows=PACK):
            nc.sync.dma_start(
                out=dst[:, c * PACK + first : c * PACK + first + n_rows, :],
                in_=src[c * K_PASS : (c + 1) * K_PASS, :].rearrange("(p j) w -> p j w", j=PACK)[
                    :, first : first + n_rows, :
                ],
            )

        gt_codes = resident.tile([P, PASSES, N_TILES, N_TILE], U32, name="gt_codes", align_bytes=64)
        gt_scales = resident.tile([P, PASSES, N_TILES, N_TILE], U8, name="gt_scales", align_bytes=64)
        dg_codes = resident.tile([P, H_BLOCKS, PASSES, GATES, M_TILE], U32, name="dg_codes", align_bytes=64)
        dg_scales = resident.tile([P, H_BLOCKS, PASSES, GATES, M_TILE], U8, name="dg_scales", align_bytes=64)

        def new_gt_grouped():
            return gt_grouped_pool.tile([P, N_TILE, PACK], BF16, name="gt_grouped", align_bytes=64)

        def regroup_gt(copy, gt_grouped, c, s, first, width):
            at = first_cols[s] % N_TILE + first
            copy(
                out=by_column_grouped(gt_grouped[:, at : at + width, :]),
                in_=by_column(stream_sb[s][:, c * PACK : (c + 1) * PACK, first : first + width]),
            )

        def regroup_tile(copy, c, n):
            gt_grouped = new_gt_grouped()
            for s in streams_of(n):
                regroup_gt(copy, gt_grouped, c, s, 0, widths[s])
            return gt_grouped

        def regroup_on_tensor(c, s):
            banks = []
            for first in range(0, N_TILE, N_TILE // 2):
                bank = psum.tile([P, N_TILE // 2, PACK], BF16, name="acc")
                for t in range(0, PACK, 2):
                    nc.tensor.matmul(
                        out=bank[:, :, t : t + 2].rearrange("p w t -> p t w"),
                        lhsT=identity_bf16[:],
                        rhs=stream_sb[s][:, c * PACK + t : c * PACK + t + 2, first : first + N_TILE // 2],
                        start=True,
                        stop=True,
                    )
                banks.append(bank)
            return banks

        def copy_bank(gt_grouped, banks, k):
            nc.scalar.copy(out=gt_grouped[:, k * (N_TILE // 2) : (k + 1) * (N_TILE // 2), :], in_=banks[k][:])

        def regrouped(banks):
            gt_grouped = new_gt_grouped()
            for k in range(len(banks)):
                copy_bank(gt_grouped, banks, k)
            return gt_grouped

        def quantise_gt(c, n, gt_grouped):
            nc.vector.quantize_mx(
                out=gt_codes[:, c, n, :].bitcast(E4M3_X4),
                scales=gt_scales[:, c, n, :],
                in_=gt_grouped[:].rearrange("p w t -> p (w t)"),
            )

        names = ("si", "tg", "sf", "so", "tg2", "ip", "fp", "minus_i", "go_so", "minus_tc", "tc2")
        si, tg, sf, so, tg2, ip, fp, minus_i, go_so, minus_tc, tc2 = [
            resident.tile([P, H_BLOCKS, ROWS, M_TILE], F32, name=name) for name in names
        ]
        minus_f, minus_g, minus_do_tc, minus_dc2 = sf, tg2, so, tc2
        dg_grouped = [
            dg_grouped_pool.tile([P, PASSES, GATES, M_TILE, PACK], BF16, name="dg_grouped", align_bytes=64)
            for hb in range(H_BLOCKS)
        ]

        def part(t, hb, r):
            return t[:, :, r, :] if hb is None else t[:, hb, r, :]

        def part_of_rows(t, hb, r, first=0):
            if hb is None:
                return t[:, r, first : first + H].rearrange("p r (b m) -> p b r m", m=M_TILE)
            return t[:, r, first + hb * M_TILE : first + (hb + 1) * M_TILE]

        def activate(out_tile, gate, func, hb, r):
            nc.scalar.activation(out=part(out_tile, hb, r), in_=part_of_rows(gf_sb, hb, r, gate * H), func=func)

        def square(out_tile, in_tile, hb, r):
            nc.scalar.activation(out=part(out_tile, hb, r), in_=part(in_tile, hb, r), func=FUNC.Square)

        def gate_activations(hb, r):
            activate(si, GATE_I, FUNC.Sigmoid, hb, r)
            activate(tg, GATE_G, FUNC.Tanh, hb, r)
            activate(sf, GATE_F, FUNC.Sigmoid, hb, r)
            square(tg2, tg, hb, r)
            activate(so, GATE_O, FUNC.Sigmoid, hb, r)

        def product(out, in0, in1):
            nc.vector.tensor_tensor(out=out, in0=in0, in1=in1, op=ALU.mult)

        def minus_one_times(out, in0, in1):
            nc.vector.scalar_tensor_tensor(out=out, in0=in0, scalar=1.0, in1=in1, op0=ALU.subtract, op1=ALU.mult)

        def make_ip(hb, r):
            product(part(ip, hb, r), part(si, hb, r), part(tg, hb, r))

        def make_fp(hb, r):
            product(part(fp, hb, r), part(sf, hb, r), part_of_rows(cell_sb, hb, r))

        def make_go_so(hb, r):
            product(part(go_so, hb, r), part(so, hb, r), part_of_rows(go_sb, hb, r))

        def make_minus_i(hb, r):
            minus_one_times(part(minus_i, hb, r), part(si, hb, r), part(ip, hb, r))

        def make_minus_f(hb, r):
            minus_one_times(part(minus_f, hb, r), part(sf, hb, r), part(fp, hb, r))

        def make_minus_g(hb, r):
            minus_one_times(part(minus_g, hb, r), part(tg2, hb, r), part(si, hb, r))

        def make_minus_do_tc(hb, r):
            minus_one_times(part(minus_do_tc, hb, r), part(so, hb, r), part(go_so, hb, r))

        def make_minus_dc2(hb, r):
            minus_one_times(part(minus_dc2, hb, r), part(tc2, hb, r), part(go_so, hb, r))

        def cell_sum(hb, r):
            nc.vector.tensor_tensor(out=part(minus_tc, hb, r), in0=part(ip, hb, r), in1=part(fp, hb, r), op=ALU.add)
            return part(minus_tc, hb, r)

        def cell_sum_on_tensor(hb, r):
            c2 = psum.tile([P, PACK, M_TILE], F32, name="acc")
            nc.tensor.matmul(out=c2[:], lhsT=identity[:], rhs=part(ip, hb, r), start=True, stop=False)
            nc.tensor.matmul(out=c2[:], lhsT=identity[:], rhs=part(fp, hb, r), start=False, stop=True)
            return c2

        def cell_tanh(hb, r, c2):
            nc.scalar.activation(out=part(minus_tc, hb, r), in_=c2, func=FUNC.Tanh, scale=-1.0)

        last_product = {
            GATE_O: (minus_do_tc, minus_tc),
            GATE_I: (minus_i, minus_dc2),
            GATE_F: (minus_f, minus_dc2),
            GATE_G: (minus_g, minus_dc2),
        }

        def finish(hb, g, c):
            in0, in1 = last_product[g]
            r = slice(c * PACK, (c + 1) * PACK)
            nc.vector.tensor_tensor(
                out=by_column_grouped(dg_grouped[hb][:, c, g, :, :]),
                in0=by_column(part(in0, hb, r)),
                in1=by_column(part(in1, hb, r)),
                op=ALU.mult,
            )

        def quantise_dg(hb, c, gates):
            nc.vector.quantize_mx(
                out=dg_codes[:, hb, c, gates, :].rearrange("p g m -> p (g m)").bitcast(E5M2_X4),
                scales=dg_scales[:, hb, c, gates, :].rearrange("p g m -> p (g m)"),
                in_=dg_grouped[hb][:, c, gates, :, :].rearrange("p g m t -> p (g m t)"),
            )

        def new_acc():
            return psum.tile([M_TILE, N_TILE], F32, name="acc")

        def multiply(acc, hb, g, n, c):
            nc.tensor.matmul_mx(
                out=acc[:],
                lhsT=dg_codes[:, hb, c, g, :].bitcast(E5M2_X4),
                lhsT_scale=dg_scales[:, hb, c, g, :],
                rhs=gt_codes[:, c, n, :].bitcast(E4M3_X4),
                rhs_scale=gt_scales[:, c, n, :],
                start=(c == 0),
                stop=(c == PASSES - 1),
            )

        def store(copy, acc, hb, g, n):
            first_row = g * H + hb * M_TILE
            result = stage.tile([M_TILE, N_TILE], F32, name="result")
            copy(out=result[:], in_=acc[:])
            nc.sync.dma_start(out=out[first_row : first_row + M_TILE, n * N_TILE : (n + 1) * N_TILE], in_=result[:])

        def products_of(hb, g, n):
            acc = new_acc()
            for c in range(PASSES):
                multiply(acc, hb, g, n, c)
            return acc

        by_pass = [slice(c * PACK, (c + 1) * PACK) for c in range(PASSES)]
        act = nc.scalar.copy
        vec = nc.vector.tensor_copy

        def load_gt(c, n):
            for s in streams_of(n):
                load(stream_sb[s], streams[s], c)

        def rows(first, n):
            return slice(first, first + n)

        def load_gf(first, n):
            load(gf_sb, gf, first // PACK, first % PACK, n)

        def cell_activations(hb, r):
            activate(si, GATE_I, FUNC.Sigmoid, hb, r)
            activate(tg, GATE_G, FUNC.Tanh, hb, r)
            activate(sf, GATE_F, FUNC.Sigmoid, hb, r)

        def output_activations(hb, r):
            activate(so, GATE_O, FUNC.Sigmoid, hb, r)
            square(tg2, tg, hb, r)

        load_gf(0, 1)
        load(cell_sb, c0[0, :, :], 0, 0, 2)
        load_gf(1, 1)
        load_gf(2, 2)
        load(cell_sb, c0[0, :, :], 0, 2, 2)
        load(go_sb, grad_out[:, 0:H], 0)
        load_gf(4, 2)
        load(cell_sb, c0[0, :, :], 1)
        load_gf(6, 2)
        load_gt(0, 0)
        load(go_sb, grad_out[:, 0:H], 1)
        load_gt(1, 0)
        for n in (1, 2):
            for c in range(PASSES):
                load_gt(c, n)

        for first in range(2):
            r = rows(first, 1)
            cell_activations(None, r)
            make_ip(None, r)
            make_fp(None, r)
            make_minus_i(None, r)
            make_minus_f(None, r)
        output_activations(None, rows(0, 2))
        make_minus_g(None, rows(0, 2))
        cell_activations(0, rows(2, 2))
        output_activations(0, rows(2, 2))
        make_ip(0, rows(2, 2))
        make_fp(0, rows(2, 2))
        make_minus_i(0, rows(2, 2))
        c2_00 = cell_sum(0, by_pass[0])
        make_minus_f(0, rows(2, 2))
        make_go_so(0, by_pass[0])
        make_minus_g(0, rows(2, 2))
        make_minus_do_tc(0, by_pass[0])
        cell_activations(1, rows(2, 2))
        cell_tanh(0, by_pass[0], c2_00)
        activate(si, GATE_I, FUNC.Sigmoid, 0, rows(4, 2))
        square(tc2, minus_tc, 0, by_pass[0])
        make_go_so(1, rows(0, 2))
        finish(0, GATE_O, 0)
        make_minus_dc2(0, by_pass[0])
        activate(tg, GATE_G, FUNC.Tanh, 0, rows(4, 2))
        activate(sf, GATE_F, FUNC.Sigmoid, 0, rows(4, 2))
        output_activations(0, rows(4, 2))
        make_ip(0, rows(4, 2))
        for g in FINISH_ORDER[1:]:
            finish(0, g, 0)
        output_activations(1, rows(2, 2))
        cell_activations(0, rows(6, 2))
        output_activations(0, rows(6, 2))
        make_fp(0, rows(4, 2))
        quantise_dg(0, 0, slice(0, GATES))
        make_ip(0, rows(6, 2))
        make_fp(0, rows(6, 2))
        make_minus_g(0, by_pass[1])
        c2_01 = cell_sum(0, by_pass[1])
        b00 = regroup_on_tensor(0, 0)
        g00 = new_gt_grouped()
        cell_activations(1, by_pass[1])
        output_activations(1, by_pass[1])
        cell_tanh(0, by_pass[1], c2_01)
        copy_bank(g00, b00, 0)
        square(tc2, minus_tc, 0, by_pass[1])
        copy_bank(g00, b00, 1)
        make_go_so(0, by_pass[1])
        make_minus_i(0, by_pass[1])
        make_minus_do_tc(0, by_pass[1])
        make_minus_f(0, by_pass[1])
        make_ip(1, rows(2, 2))
        finish(0, GATE_O, 1)
        make_fp(1, rows(2, 2))
        make_minus_dc2(0, by_pass[1])
        quantise_gt(0, 0, g00)
        g10 = regrouped(regroup_on_tensor(1, 0))
        for g in FINISH_ORDER[1:]:
            finish(0, g, 1)
        quantise_gt(1, 0, g10)
        quantise_dg(0, 1, slice(0, GATES))

        g01 = regrouped(regroup_on_tensor(0, 1))
        c2_10 = cell_sum_on_tensor(1, by_pass[0])
        g11 = regroup_tile(act, 1, 1)
        acc0 = [products_of(0, g, 0) for g in FINISH_ORDER]
        make_ip(1, by_pass[1])
        make_fp(1, by_pass[1])
        make_minus_g(1, rows(2, 2))
        for g, acc in zip(FINISH_ORDER, acc0):
            store(act, acc, 0, g, 0)
        quantise_gt(0, 1, g01)
        quantise_gt(1, 1, g11)
        acc1 = [products_of(0, g, 1) for g in FINISH_ORDER]
        c2_11 = cell_sum_on_tensor(1, by_pass[1])
        g02 = regroup_tile(vec, 0, 2)
        g12 = regroup_tile(act, 1, 2)
        make_minus_i(1, rows(2, ROWS - 2))
        quantise_gt(0, 2, g02)
        cell_tanh(1, by_pass[0], c2_10[:])
        for k, (g, acc) in enumerate(zip(FINISH_ORDER, acc1)):
            store(act, acc, 0, g, 1)
            if k == 0:
                square(tc2, minus_tc, 1, by_pass[0])
            if k == 2:
                cell_tanh(1, by_pass[1], c2_11[:])
        square(tc2, minus_tc, 1, by_pass[1])
        make_go_so(1, rows(2, ROWS - 2))
        quantise_gt(1, 2, g12)
        make_minus_do_tc(1, by_pass[0])
        make_minus_do_tc(1, by_pass[1])
        for g in FINISH_ORDER:
            store(act, products_of(0, g, 2), 0, g, 2)

        accs = {}

        def multiply_last(g, c):
            if c == 0:
                accs[g] = [new_acc() for n in range(N_TILES)]
            for n in range(N_TILES):
                multiply(accs[g][n], 1, g, n, c)

        def quantise_and_multiply(g, c):
            quantise_dg(1, c, slice(g, g + 1))
            multiply_last(g, c)

        def store_last(g):
            for n in range(N_TILES):
                store(vec if g == FINISH_ORDER[-1] and n != 1 else act, accs[g][n], 1, g, n)

        finish(1, GATE_O, 0)
        make_minus_dc2(1, by_pass[0])
        quantise_and_multiply(GATE_O, 0)
        make_minus_f(1, rows(2, ROWS - 2))
        finish(1, GATE_O, 1)
        make_minus_dc2(1, by_pass[1])
        quantise_and_multiply(GATE_O, 1)
        store_last(GATE_O)
        finish(1, GATE_I, 0)
        finish(1, GATE_I, 1)
        quantise_and_multiply(GATE_I, 0)
        quantise_and_multiply(GATE_I, 1)
        store_last(GATE_I)
        finish(1, GATE_F, 0)
        finish(1, GATE_F, 1)
        quantise_and_multiply(GATE_F, 0)
        finish(1, GATE_G, 0)
        quantise_and_multiply(GATE_F, 1)
        store_last(GATE_F)
        make_minus_g(1, by_pass[1])
        quantise_and_multiply(GATE_G, 0)
        finish(1, GATE_G, 1)
        quantise_and_multiply(GATE_G, 1)
        store_last(GATE_G)
